import numpy as np
import ml_dtypes


def mxq(x, axis, fmt="e4m3"):
    dtype, down = {"e4m3": (ml_dtypes.float8_e4m3fn, 7), "e5m2": (ml_dtypes.float8_e5m2, 14)}[fmt]
    v = np.moveaxis(np.asarray(x, np.float32).astype(ml_dtypes.bfloat16).astype(np.float64), axis, -1)
    blocks = v.reshape(v.shape[:-1] + (-1, 32))
    amax = np.abs(blocks).max(-1, keepdims=True)
    byte = np.maximum(np.where(amax > 0, np.frexp(amax)[1] - 1 + 127, 0) - down, 1)
    scale = np.exp2(byte - 127.0)
    codes = (blocks / scale).astype(np.float32).astype(dtype).astype(np.float64)
    return np.moveaxis((codes * scale).reshape(v.shape), -1, axis)


WIDE = False


def mx_kscale(k):
    if not WIDE:
        return np.ones(k)
    levels = np.array([10, -10, 5, -5, 0])
    a = np.random.permutation(np.resize(levels, k // 512 * 4)).reshape(k // 512, 4)
    idx = np.arange(k)
    return np.exp2(a[idx // 512, idx % 128 // 32])


BF16 = ml_dtypes.bfloat16


def bf(x):
    return np.asarray(x, np.float32).astype(BF16)


def f64(x):
    return np.asarray(x).astype(np.float64)


E2M1 = np.array([0.0, 0.5, 1.0, 1.5, 2.0, 3.0, 4.0, 6.0, -0.0, -0.5, -1.0, -1.5, -2.0, -3.0, -4.0, -6.0])


def pack_weight(w, fmt):
    k, n = w.shape
    w = f64(bf(w)).reshape(k // 32, 32, n)
    amax = np.abs(w).max(1)
    if fmt == "e4m3":
        byte = np.frexp(amax)[1] - 1 + 127 - 7
    else:
        mant, ex = np.frexp(amax / 6.0)
        byte = np.where(mant > 0.5, ex, ex - 1) + 127
    byte = np.clip(np.where(amax > 0, byte, 1), 1, 254)
    scaled = (w * np.exp2(127.0 - byte)[:, None, :]).reshape(k, n).astype(np.float32)
    by_word = np.ascontiguousarray(scaled.reshape(k // 512, 128, 4, n).transpose(0, 1, 3, 2))
    if fmt == "e4m3":
        words = by_word.astype(ml_dtypes.float8_e4m3fn).view(np.uint8)
    else:
        c = by_word.astype(ml_dtypes.float4_e2m1fn).view(np.uint8) & 0xF
        words = c[..., 0::2] | (c[..., 1::2] << 4)
    return np.ascontiguousarray(words), np.ascontiguousarray(byte.astype(np.uint8).reshape(k // 512, 16, n))


def unpack_weight(words, scales, fmt):
    g, p, n, _ = words.shape
    if fmt == "e4m3":
        vals = np.ascontiguousarray(words).view(ml_dtypes.float8_e4m3fn).astype(np.float64)
    else:
        nib = np.empty((g, p, n, 4), np.uint8)
        nib[..., 0::2] = words & 0xF
        nib[..., 1::2] = words >> 4
        vals = E2M1[nib]
    vals = vals * np.repeat(np.exp2(scales.astype(np.float64) - 127.0), 8, axis=1)[..., None]
    return vals.transpose(0, 1, 3, 2).reshape(g * 512, n)

def pack4(w):
    words, scales = pack_weight(w, "e2m1")
    return words.reshape(words.shape[0], 128, -1), scales


def unpack4(words, scales):
    return unpack_weight(words.reshape(words.shape[0], 128, -1, 2), scales, "e2m1")


B, C, W, H = 8, 1024, 8, 16


def spatial_shift1(y):
    cq = y.shape[-1] // 4
    p0 = np.concatenate([y[:, :1, :, 0 * cq:1 * cq], y[:, :-1, :, 0 * cq:1 * cq]], axis=1)
    p1 = np.concatenate([y[:, 1:, :, 1 * cq:2 * cq], y[:, -1:, :, 1 * cq:2 * cq]], axis=1)
    p2 = np.concatenate([y[:, :, :1, 2 * cq:3 * cq], y[:, :, :-1, 2 * cq:3 * cq]], axis=2)
    p3 = np.concatenate([y[:, :, 1:, 3 * cq:], y[:, :, -1:, 3 * cq:]], axis=2)
    return np.concatenate([p0, p1, p2, p3], axis=-1)


def spatial_shift2(y):
    cq = y.shape[-1] // 4
    p0 = np.concatenate([y[:, :, :1, 0 * cq:1 * cq], y[:, :, :-1, 0 * cq:1 * cq]], axis=2)
    p1 = np.concatenate([y[:, :, 1:, 1 * cq:2 * cq], y[:, :, -1:, 1 * cq:2 * cq]], axis=2)
    p2 = np.concatenate([y[:, :1, :, 2 * cq:3 * cq], y[:, :-1, :, 2 * cq:3 * cq]], axis=1)
    p3 = np.concatenate([y[:, 1:, :, 3 * cq:], y[:, -1:, :, 3 * cq:]], axis=1)
    return np.concatenate([p0, p1, p2, p3], axis=-1)


def setup_inputs():
    s = mx_kscale(C)
    x = bf(np.random.standard_normal((B, C, W, H)) * s[None, :, None, None])
    w1 = np.random.standard_normal((3 * C, C)) / np.sqrt(C) / s[None, :]
    w1_words, w1_scales = pack4(np.ascontiguousarray(w1.T))
    b1 = bf(np.random.standard_normal(3 * C) * 0.1)
    return {"x": x, "w1_words": w1_words, "w1_scales": w1_scales, "b1": b1}


def reference(x, w1_words, w1_scales, b1):
    xp = f64(x).transpose(0, 2, 3, 1)
    y = (mxq(xp, 3, "e4m3") @ unpack4(w1_words, w1_scales)) + f64(b1)
    x1 = spatial_shift1(y[..., :C])
    x2 = spatial_shift2(y[..., C:2 * C])
    x3 = y[..., 2 * C:]
    a = np.sum(x1 + x2 + x3, axis=(1, 2))
    return x1, x2, x3, a

@@ -1,0 +1,155 @@
+from contextlib import ExitStack
+
+import concourse.mybir as mybir
+
+F32 = mybir.dt.float32
+BF16 = mybir.dt.bfloat16
+I32 = mybir.dt.int32
+U32 = mybir.dt.uint32
+U8 = mybir.dt.uint8
+FP8X4 = mybir.dt.float8_e4m3fn_x4
+FP4X4 = mybir.dt.float4_e2m1fn_x4
+ADD = mybir.AluOpType.add
+
+P = 128
+PACK = 4
+B, C, W, H = 8, 1024, 8, 16
+T = W * H
+G = C // (P * PACK)
+BRANCHES = 3
+O = BRANCHES * C
+QUARTER = C // 4
+BANK = 512
+PIECE = 128
+
+FLOPS = 2 * B * T * C * O
+
+SAME, W_MINUS, W_PLUS, H_MINUS, H_PLUS = range(5)
+SHIFT_OF_QUARTER = (
+    (W_MINUS, W_PLUS, H_MINUS, H_PLUS),
+    (H_MINUS, H_PLUS, W_MINUS, W_PLUS),
+    (SAME, SAME, SAME, SAME),
+)
+
+
+def tile_modelnew_pa_kernel(tc, x, w1_words, w1_scales, b1, out_0, out_1, out_2, out_3):
+    nc = tc.nc
+    outs = (out_0, out_1, out_2)
+
+    with ExitStack() as ctx:
+        keep = ctx.enter_context(tc.tile_pool(name="keep", bufs=1))
+        stage = ctx.enter_context(tc.tile_pool(name="stage", bufs=2))
+        results = ctx.enter_context(tc.tile_pool(name="results", bufs=3))
+        banks = ctx.enter_context(tc.psum_pool(name="banks", bufs=6))
+        pooled = ctx.enter_context(tc.psum_pool(name="pooled", bufs=1))
+
+        raw = keep.tile([P, B, G, PACK, T], BF16)
+        w_words = keep.tile([P, G, 2 * O], U8, align_bytes=64)
+        w_planes = keep.tile([P, G, O], U8, align_bytes=64)
+        bias_rows = keep.tile([P, O], BF16)
+        x_words = [keep.tile([P, B, G, T], U32, align_bytes=64, name="x_words%d" % v) for v in range(5)]
+        x_planes = [keep.tile([P, B, G, T], U8, align_bytes=64, name="x_planes%d" % v) for v in range(5)]
+        pick = keep.tile([P, 2 * P - 1], F32)
+        a_rows = keep.tile([P, C], F32)
+
+        nc.vector.memset(w_planes[:].bitcast(I32), 0)
+        nc.vector.memset(pick[:], 0.0)
+        nc.vector.memset(pick[:, P - 1 : P], 1.0)
+
+        def load_x(b):
+            nc.sync.dma_start(
+                out=raw[:, b],
+                in_=x[b].rearrange("(g p j) w h -> p g j (w h)", g=G, p=P, j=PACK),
+            )
+
+        load_x(0)
+        for g in range(G):
+            for first in range(8):
+                low_q, r = divmod(first, 4)
+                nc.sync.dma_start(
+                    out=w_planes[32 * low_q + r : P : 64, g, :].bitcast(I32),
+                    in_=w1_scales[g, 4 * low_q + r : 16 : 8, :].bitcast(I32),
+                )
+        nc.scalar.dma_start(out=bias_rows[:], in_=b1.partition_broadcast(P))
+        for branch in range(BRANCHES):
+            cols = slice(2 * C * branch, 2 * C * (branch + 1))
+            nc.sync.dma_start(
+                out=w_words[:, :, cols].bitcast(I32),
+                in_=w1_words.rearrange("g p n -> p g n")[:, :, cols].bitcast(I32),
+            )
+        for b in range(1, B):
+            load_x(b)
+
+        a_sums = [pooled.tile([P, BANK], F32, name="a_sums%d" % half) for half in range(C // BANK)]
+
+        for b in range(B):
+            padded = stage.tile([P, G, T + 2 * H, PACK], BF16, align_bytes=64)
+            by_token = raw[:, b].rearrange("p g j t -> p g t j")
+            nc.scalar.copy(out=padded[:, :, H : H + T, :], in_=by_token)
+            nc.scalar.copy(out=padded[:, :, 0:H, :], in_=by_token[:, :, 0:H, :])
+            nc.scalar.copy(out=padded[:, :, H + T : 2 * H + T, :], in_=by_token[:, :, T - H : T, :])
+            grid = padded[:, :, H : H + T, :].rearrange("p g (w h) j -> p g w h j", h=H)
+            h_minus = stage.tile([P, G, W, H, PACK], BF16, align_bytes=64)
+            nc.scalar.copy(out=h_minus[:, :, :, 1:H, :], in_=grid[:, :, :, 0 : H - 1, :])
+            nc.scalar.copy(out=h_minus[:, :, :, 0:1, :], in_=grid[:, :, :, 0:1, :])
+            h_plus = stage.tile([P, G, W, H, PACK], BF16, align_bytes=64)
+            nc.scalar.copy(out=h_plus[:, :, :, 0 : H - 1, :], in_=grid[:, :, :, 1:H, :])
+            nc.scalar.copy(out=h_plus[:, :, :, H - 1 : H, :], in_=grid[:, :, :, H - 1 : H, :])
+
+            for g in range(G):
+                for version, start in ((SAME, H), (W_MINUS, 0), (W_PLUS, 2 * H)):
+                    nc.vector.quantize_mx(
+                        out=x_words[version][:, b, g, :].bitcast(FP8X4),
+                        scales=x_planes[version][:, b, g, :],
+                        in_=padded[:, g, start : start + T, :].rearrange("p t j -> p (t j)"),
+                    )
+            for version, shifted in ((H_MINUS, h_minus), (H_PLUS, h_plus)):
+                nc.vector.quantize_mx(
+                    out=x_words[version][:, b].rearrange("p g t -> p (g t)").bitcast(FP8X4),
+                    scales=x_planes[version][:, b].rearrange("p g t -> p (g t)"),
+                    in_=shifted[:].rearrange("p g w h j -> p (g w h j)"),
+                )
+
+            y = []
+            for branch in range(BRANCHES):
+                y_branch = results.tile([P, C], F32, name="y%d" % branch)
+                y.append(y_branch)
+                width = BANK if branch == 2 else PIECE
+                for bank_start in range(0, C, BANK):
+                    acc = banks.tile([P, BANK], F32)
+                    for c0 in range(bank_start, bank_start + BANK, width):
+                        version = SHIFT_OF_QUARTER[branch][c0 // QUARTER]
+                        o0 = branch * C + c0
+                        for g in range(G):
+                            nc.tensor.matmul_mx(
+                                out=acc[:, c0 - bank_start : c0 - bank_start + width],
+                                lhsT=x_words[version][:, b, g, :].bitcast(FP8X4),
+                                lhsT_scale=x_planes[version][:, b, g, :],
+                                rhs=w_words[:, g, 2 * o0 : 2 * (o0 + width)].bitcast(FP4X4),
+                                rhs_scale=w_planes[:, g, o0 : o0 + width],
+                                start=(g == 0),
+                                stop=(g == G - 1),
+                            )
+                    nc.vector.tensor_tensor(
+                        out=y_branch[:, bank_start : bank_start + BANK],
+                        in0=acc[:],
+                        in1=bias_rows[:, branch * C + bank_start : branch * C + bank_start + BANK],
+                        op=ADD,
+                    )
+                nc.sync.dma_start(out=outs[branch][b].rearrange("w h c -> (w h) c"), in_=y_branch[:])
+
+            z = results.tile([P, C], F32)
+            nc.gpsimd.tensor_tensor(out=z[:], in0=y[0][:], in1=y[1][:], op=ADD)
+            nc.gpsimd.tensor_tensor(out=z[:], in0=z[:], in1=y[2][:], op=ADD)
+            for half, a_sum in enumerate(a_sums):
+                nc.tensor.matmul(
+                    out=a_sum[:],
+                    lhsT=pick[:, P - 1 - b : 2 * P - 1 - b],
+                    rhs=z[:, half * BANK : (half + 1) * BANK],
+                    start=(b == 0),
+                    stop=(b == B - 1),
+                )
+
+        for half, a_sum in enumerate(a_sums):
+            nc.scalar.copy(out=a_rows[:, half * BANK : (half + 1) * BANK], in_=a_sum[:])
+        nc.sync.dma_start(out=out_3, in_=a_rows[0:B, :])

@@ -1,6 +1,7 @@
 from contextlib import ExitStack
 
 import concourse.mybir as mybir
+from concourse.masks import make_identity
 
 F32 = mybir.dt.float32
 BF16 = mybir.dt.bfloat16
@@ -10,6 +11,7 @@ U8 = mybir.dt.uint8
 FP8X4 = mybir.dt.float8_e4m3fn_x4
 FP4X4 = mybir.dt.float4_e2m1fn_x4
 ADD = mybir.AluOpType.add
+COPY = mybir.ActivationFunctionType.Copy
 
 P = 128
 PACK = 4
@@ -21,6 +23,9 @@ O = BRANCHES * C
 QUARTER = C // 4
 BANK = 512
 PIECE = 128
+BLOCKS = C // P
+TOKEN_WORDS = PACK // 2
+AHEAD = 2
 
 FLOPS = 2 * B * T * C * O
 
@@ -30,6 +35,7 @@ SHIFT_OF_QUARTER = (
     (H_MINUS, H_PLUS, W_MINUS, W_PLUS),
     (SAME, SAME, SAME, SAME),
 )
+BRANCH_ORDER = (2, 0, 1)
 
 
 def tile_modelnew_pa_kernel(tc, x, w1_words, w1_scales, b1, out_0, out_1, out_2, out_3):
@@ -38,10 +44,10 @@ def tile_modelnew_pa_kernel(tc, x, w1_words, w1_scales, b1, out_0, out_1, out_2,
 
     with ExitStack() as ctx:
         keep = ctx.enter_context(tc.tile_pool(name="keep", bufs=1))
-        stage = ctx.enter_context(tc.tile_pool(name="stage", bufs=2))
+        stage = ctx.enter_context(tc.tile_pool(name="stage", bufs=3))
         results = ctx.enter_context(tc.tile_pool(name="results", bufs=3))
-        banks = ctx.enter_context(tc.psum_pool(name="banks", bufs=6))
-        pooled = ctx.enter_context(tc.psum_pool(name="pooled", bufs=1))
+        banks = ctx.enter_context(tc.psum_pool(name="banks", bufs=4))
+        turns = ctx.enter_context(tc.psum_pool(name="turns", bufs=4))
 
         raw = keep.tile([P, B, G, PACK, T], BF16)
         w_words = keep.tile([P, G, 2 * O], U8, align_bytes=64)
@@ -49,12 +55,14 @@ def tile_modelnew_pa_kernel(tc, x, w1_words, w1_scales, b1, out_0, out_1, out_2,
         bias_rows = keep.tile([P, O], BF16)
         x_words = [keep.tile([P, B, G, T], U32, align_bytes=64, name="x_words%d" % v) for v in range(5)]
         x_planes = [keep.tile([P, B, G, T], U8, align_bytes=64, name="x_planes%d" % v) for v in range(5)]
-        pick = keep.tile([P, 2 * P - 1], F32)
-        a_rows = keep.tile([P, C], F32)
+        identity = keep.tile([P, P], F32)
+        unread = keep.tile([P, BLOCKS, 2 * P], BF16)
+        a_by_channel = keep.tile([P, P], F32)
+        a_rows = keep.tile([P, P], F32)
 
         nc.vector.memset(w_planes[:].bitcast(I32), 0)
-        nc.vector.memset(pick[:], 0.0)
-        nc.vector.memset(pick[:, P - 1 : P], 1.0)
+        nc.vector.memset(a_by_channel[:], 0.0)
+        make_identity(nc, identity[:])
 
         def load_x(b):
             nc.sync.dma_start(
@@ -62,58 +70,63 @@ def tile_modelnew_pa_kernel(tc, x, w1_words, w1_scales, b1, out_0, out_1, out_2,
                 in_=x[b].rearrange("(g p j) w h -> p g j (w h)", g=G, p=P, j=PACK),
             )
 
-        load_x(0)
-        for g in range(G):
-            for first in range(8):
-                low_q, r = divmod(first, 4)
-                nc.sync.dma_start(
-                    out=w_planes[32 * low_q + r : P : 64, g, :].bitcast(I32),
-                    in_=w1_scales[g, 4 * low_q + r : 16 : 8, :].bitcast(I32),
-                )
-        nc.scalar.dma_start(out=bias_rows[:], in_=b1.partition_broadcast(P))
-        for branch in range(BRANCHES):
-            cols = slice(2 * C * branch, 2 * C * (branch + 1))
+        def load_words(first_channel, channels):
+            cols = slice(2 * first_channel, 2 * (first_channel + channels))
             nc.sync.dma_start(
                 out=w_words[:, :, cols].bitcast(I32),
                 in_=w1_words.rearrange("g p n -> p g n")[:, :, cols].bitcast(I32),
             )
+
+        load_x(0)
+        for r in range(4):
+            nc.sync.dma_start(
+                out=w_planes[r : P : 32, :, :].bitcast(I32),
+                in_=w1_scales[:, r : 16 : 4, :].rearrange("g q n -> q g n").bitcast(I32),
+            )
+        load_words(2 * C, C)
+        nc.sync.dma_start(out=bias_rows[:], in_=b1.partition_broadcast(P))
+        load_words(0, 2 * C)
         for b in range(1, B):
             load_x(b)
 
-        a_sums = [pooled.tile([P, BANK], F32, name="a_sums%d" % half) for half in range(C // BANK)]
-
-        for b in range(B):
+        def quantise_batch(b):
             padded = stage.tile([P, G, T + 2 * H, PACK], BF16, align_bytes=64)
             by_token = raw[:, b].rearrange("p g j t -> p g t j")
             nc.scalar.copy(out=padded[:, :, H : H + T, :], in_=by_token)
             nc.scalar.copy(out=padded[:, :, 0:H, :], in_=by_token[:, :, 0:H, :])
             nc.scalar.copy(out=padded[:, :, H + T : 2 * H + T, :], in_=by_token[:, :, T - H : T, :])
-            grid = padded[:, :, H : H + T, :].rearrange("p g (w h) j -> p g w h j", h=H)
-            h_minus = stage.tile([P, G, W, H, PACK], BF16, align_bytes=64)
-            nc.scalar.copy(out=h_minus[:, :, :, 1:H, :], in_=grid[:, :, :, 0 : H - 1, :])
-            nc.scalar.copy(out=h_minus[:, :, :, 0:1, :], in_=grid[:, :, :, 0:1, :])
-            h_plus = stage.tile([P, G, W, H, PACK], BF16, align_bytes=64)
-            nc.scalar.copy(out=h_plus[:, :, :, 0 : H - 1, :], in_=grid[:, :, :, 1:H, :])
-            nc.scalar.copy(out=h_plus[:, :, :, H - 1 : H, :], in_=grid[:, :, :, H - 1 : H, :])
-
-            for g in range(G):
-                for version, start in ((SAME, H), (W_MINUS, 0), (W_PLUS, 2 * H)):
+            for version, start in ((SAME, H), (W_MINUS, 0), (W_PLUS, 2 * H)):
+                for g in range(G):
                     nc.vector.quantize_mx(
                         out=x_words[version][:, b, g, :].bitcast(FP8X4),
                         scales=x_planes[version][:, b, g, :],
                         in_=padded[:, g, start : start + T, :].rearrange("p t j -> p (t j)"),
                     )
+            row = TOKEN_WORDS * H
+            last = row - TOKEN_WORDS
+            grid = (
+                padded[:, :, H : H + T, :]
+                .rearrange("p g t j -> p g (t j)")
+                .bitcast(F32)
+                .rearrange("p g (w k) -> p g w k", k=row)
+            )
+            h_minus = stage.tile([P, G, W, H * PACK], BF16, align_bytes=64)
+            nc.scalar.copy(out=h_minus[:].bitcast(F32)[:, :, :, TOKEN_WORDS:row], in_=grid[:, :, :, 0:last])
+            nc.scalar.copy(out=h_minus[:].bitcast(F32)[:, :, :, 0:TOKEN_WORDS], in_=grid[:, :, :, 0:TOKEN_WORDS])
+            h_plus = stage.tile([P, G, W, H * PACK], BF16, align_bytes=64)
+            nc.scalar.copy(out=h_plus[:].bitcast(F32)[:, :, :, 0:last], in_=grid[:, :, :, TOKEN_WORDS:row])
+            nc.scalar.copy(out=h_plus[:].bitcast(F32)[:, :, :, last:row], in_=grid[:, :, :, last:row])
             for version, shifted in ((H_MINUS, h_minus), (H_PLUS, h_plus)):
                 nc.vector.quantize_mx(
                     out=x_words[version][:, b].rearrange("p g t -> p (g t)").bitcast(FP8X4),
                     scales=x_planes[version][:, b].rearrange("p g t -> p (g t)"),
-                    in_=shifted[:].rearrange("p g w h j -> p (g w h j)"),
+                    in_=shifted[:].rearrange("p g w k -> p (g w k)"),
                 )
 
-            y = []
-            for branch in range(BRANCHES):
-                y_branch = results.tile([P, C], F32, name="y%d" % branch)
-                y.append(y_branch)
+        def project_batch(b):
+            y = {}
+            for branch in BRANCH_ORDER:
+                y[branch] = results.tile([P, C], F32, name="y%d" % branch)
                 width = BANK if branch == 2 else PIECE
                 for bank_start in range(0, C, BANK):
                     acc = banks.tile([P, BANK], F32)
@@ -131,25 +144,50 @@ def tile_modelnew_pa_kernel(tc, x, w1_words, w1_scales, b1, out_0, out_1, out_2,
                                 stop=(g == G - 1),
                             )
                     nc.vector.tensor_tensor(
-                        out=y_branch[:, bank_start : bank_start + BANK],
+                        out=y[branch][:, bank_start : bank_start + BANK],
                         in0=acc[:],
                         in1=bias_rows[:, branch * C + bank_start : branch * C + bank_start + BANK],
                         op=ADD,
                     )
-                nc.sync.dma_start(out=outs[branch][b].rearrange("w h c -> (w h) c"), in_=y_branch[:])
+                nc.sync.dma_start(out=outs[branch][b].rearrange("w h c -> (w h) c"), in_=y[branch][:])
+                if branch == BRANCH_ORDER[1]:
+                    first_two = results.tile([P, C], F32)
+                    nc.gpsimd.tensor_tensor(
+                        out=first_two[:], in0=y[BRANCH_ORDER[0]][:], in1=y[BRANCH_ORDER[1]][:], op=ADD
+                    )
+            return first_two, y[BRANCH_ORDER[2]]
 
-            z = results.tile([P, C], F32)
-            nc.gpsimd.tensor_tensor(out=z[:], in0=y[0][:], in1=y[1][:], op=ADD)
-            nc.gpsimd.tensor_tensor(out=z[:], in0=z[:], in1=y[2][:], op=ADD)
-            for half, a_sum in enumerate(a_sums):
-                nc.tensor.matmul(
-                    out=a_sum[:],
-                    lhsT=pick[:, P - 1 - b : 2 * P - 1 - b],
-                    rhs=z[:, half * BANK : (half + 1) * BANK],
-                    start=(b == 0),
-                    stop=(b == B - 1),
-                )
+        def sum_tokens(b, parts):
+            for i in range(0, BLOCKS, 2):
+                turned = turns.tile([P, 2, 2, P], F32)
+                for k in range(2):
+                    for n, part in enumerate(parts):
+                        nc.tensor.transpose(turned[:, k, n, :], part[:, (i + k) * P : (i + k + 1) * P], identity[:])
+                for k in range(2):
+                    nc.scalar.activation(
+                        out=unread[:, i + k, :],
+                        in_=turned[:, k].rearrange("p n t -> p (n t)"),
+                        func=COPY,
+                        accum_out=a_by_channel[:, b * BLOCKS + i + k : b * BLOCKS + i + k + 1],
+                    )
 
-        for half, a_sum in enumerate(a_sums):
-            nc.scalar.copy(out=a_rows[:, half * BANK : (half + 1) * BANK], in_=a_sum[:])
-        nc.sync.dma_start(out=out_3, in_=a_rows[0:B, :])
+        ctx.enter_context(tc.manual_schedule())
+        for b in range(AHEAD):
+            quantise_batch(b)
+        parts_before = None
+        for b in range(B):
+            if b + AHEAD < B:
+                quantise_batch(b + AHEAD)
+            parts = project_batch(b)
+            if parts_before is not None:
+                sum_tokens(b - 1, parts_before)
+            parts_before = parts
+        sum_tokens(B - 1, parts_before)
+
+        a_turned = turns.tile([P, P], F32, tag="turned")
+        nc.tensor.transpose(a_turned[:], a_by_channel[:], identity[:])
+        nc.scalar.copy(out=a_rows[:], in_=a_turned[:])
+        nc.sync.dma_start(
+            out=out_3.rearrange("b (i c) -> (b i) c", c=P),
+            in_=a_rows[0 : B * BLOCKS, :],
+        )

@@ -18,45 +18,45 @@ PACK = 4
 B, C, W, H = 8, 1024, 8, 16
 T = W * H
 G = C // (P * PACK)
-BRANCHES = 3
-O = BRANCHES * C
+O = 3 * C
 QUARTER = C // 4
 BANK = 512
-PIECE = 128
 BLOCKS = C // P
 TOKEN_WORDS = PACK // 2
 AHEAD = 2
+LATE = 2
 
 FLOPS = 2 * B * T * C * O
 
-SAME, W_MINUS, W_PLUS, H_MINUS, H_PLUS = range(5)
-SHIFT_OF_QUARTER = (
-    (W_MINUS, W_PLUS, H_MINUS, H_PLUS),
-    (H_MINUS, H_PLUS, W_MINUS, W_PLUS),
-    (SAME, SAME, SAME, SAME),
-)
-BRANCH_ORDER = (2, 0, 1)
+W_MINUS, W_PLUS, H_MINUS, H_PLUS, SAME = range(5)
+SHIFTS = (W_MINUS, W_PLUS, H_MINUS, H_PLUS)
+
+
+def x2_quarter(shift):
+    return (shift + 2) % 4
 
 
 def tile_modelnew_pa_kernel(tc, x, w1_words, w1_scales, b1, out_0, out_1, out_2, out_3):
     nc = tc.nc
-    outs = (out_0, out_1, out_2)
 
     with ExitStack() as ctx:
         keep = ctx.enter_context(tc.tile_pool(name="keep", bufs=1))
         stage = ctx.enter_context(tc.tile_pool(name="stage", bufs=3))
         results = ctx.enter_context(tc.tile_pool(name="results", bufs=3))
-        banks = ctx.enter_context(tc.psum_pool(name="banks", bufs=4))
-        turns = ctx.enter_context(tc.psum_pool(name="turns", bufs=4))
+        sums = ctx.enter_context(tc.tile_pool(name="sums", bufs=LATE + 2))
+        banks = ctx.enter_context(tc.psum_pool(name="banks", bufs=6))
+        turns = ctx.enter_context(tc.psum_pool(name="turns", bufs=2))
 
         raw = keep.tile([P, B, G, PACK, T], BF16)
-        w_words = keep.tile([P, G, 2 * O], U8, align_bytes=64)
         w_planes = keep.tile([P, G, O], U8, align_bytes=64)
-        bias_rows = keep.tile([P, O], BF16)
+        x3_words = keep.tile([P, G, 2 * C], U8, align_bytes=64)
+        pair_words = keep.tile([P, G, 4, 2, 2 * QUARTER], U8, align_bytes=64)
+        pair_planes = keep.tile([P, G, 4, 2, QUARTER], U8, align_bytes=64)
+        bias_rows = keep.tile([P, O // QUARTER, QUARTER], BF16)
         x_words = [keep.tile([P, B, G, T], U32, align_bytes=64, name="x_words%d" % v) for v in range(5)]
         x_planes = [keep.tile([P, B, G, T], U8, align_bytes=64, name="x_planes%d" % v) for v in range(5)]
         identity = keep.tile([P, P], F32)
-        unread = keep.tile([P, BLOCKS, 2 * P], BF16)
+        unread = keep.tile([P, BLOCKS, P], BF16)
         a_by_channel = keep.tile([P, P], F32)
         a_rows = keep.tile([P, P], F32)
 
@@ -70,24 +70,43 @@ def tile_modelnew_pa_kernel(tc, x, w1_words, w1_scales, b1, out_0, out_1, out_2,
                 in_=x[b].rearrange("(g p j) w h -> p g j (w h)", g=G, p=P, j=PACK),
             )
 
-        def load_words(first_channel, channels):
-            cols = slice(2 * first_channel, 2 * (first_channel + channels))
-            nc.sync.dma_start(
-                out=w_words[:, :, cols].bitcast(I32),
-                in_=w1_words.rearrange("g p n -> p g n")[:, :, cols].bitcast(I32),
-            )
-
         load_x(0)
         for r in range(4):
             nc.sync.dma_start(
                 out=w_planes[r : P : 32, :, :].bitcast(I32),
                 in_=w1_scales[:, r : 16 : 4, :].rearrange("g q n -> q g n").bitcast(I32),
             )
-        load_words(2 * C, C)
-        nc.sync.dma_start(out=bias_rows[:], in_=b1.partition_broadcast(P))
-        load_words(0, 2 * C)
-        for b in range(1, B):
+        nc.sync.dma_start(
+            out=x3_words[:].bitcast(I32),
+            in_=w1_words.rearrange("g p n -> p g n")[:, :, 4 * C : 6 * C].bitcast(I32),
+        )
+        nc.sync.dma_start(out=bias_rows[:].rearrange("p q c -> p (q c)"), in_=b1.partition_broadcast(P))
+        load_x(1)
+        for g in range(G):
+            nc.sync.dma_start(
+                out=pair_words[:, g, :, 0, :].bitcast(I32),
+                in_=w1_words[g, :, 0 : 2 * C].rearrange("p (s k) -> p s k", s=4).bitcast(I32),
+            )
+            for shift in (0, 2):
+                first = 2 * (C + x2_quarter(shift) * QUARTER)
+                nc.sync.dma_start(
+                    out=pair_words[:, g, shift : shift + 2, 1, :].bitcast(I32),
+                    in_=w1_words[g, :, first : first + 4 * QUARTER].rearrange("p (s k) -> p s k", s=2).bitcast(I32),
+                )
+        for b in range(2, B):
             load_x(b)
+
+        def pair_scale_bytes():
+            nc.vector.tensor_copy(
+                out=pair_planes[:, :, :, 0, :].bitcast(I32),
+                in_=w_planes[:, :, 0:C].rearrange("p g (s c) -> p g s c", s=4).bitcast(I32),
+            )
+            for shift in (0, 2):
+                first = C + x2_quarter(shift) * QUARTER
+                nc.vector.tensor_copy(
+                    out=pair_planes[:, :, shift : shift + 2, 1, :].bitcast(I32),
+                    in_=w_planes[:, :, first : first + 2 * QUARTER].rearrange("p g (s c) -> p g s c", s=2).bitcast(I32),
+                )
 
         def quantise_batch(b):
             padded = stage.tile([P, G, T + 2 * H, PACK], BF16, align_bytes=64)
@@ -123,66 +142,90 @@ def tile_modelnew_pa_kernel(tc, x, w1_words, w1_scales, b1, out_0, out_1, out_2,
                     in_=shifted[:].rearrange("p g w k -> p (g w k)"),
                 )
 
-        def project_batch(b):
-            y = {}
-            for branch in BRANCH_ORDER:
-                y[branch] = results.tile([P, C], F32, name="y%d" % branch)
-                width = BANK if branch == 2 else PIECE
-                for bank_start in range(0, C, BANK):
-                    acc = banks.tile([P, BANK], F32)
-                    for c0 in range(bank_start, bank_start + BANK, width):
-                        version = SHIFT_OF_QUARTER[branch][c0 // QUARTER]
-                        o0 = branch * C + c0
-                        for g in range(G):
-                            nc.tensor.matmul_mx(
-                                out=acc[:, c0 - bank_start : c0 - bank_start + width],
-                                lhsT=x_words[version][:, b, g, :].bitcast(FP8X4),
-                                lhsT_scale=x_planes[version][:, b, g, :],
-                                rhs=w_words[:, g, 2 * o0 : 2 * (o0 + width)].bitcast(FP4X4),
-                                rhs_scale=w_planes[:, g, o0 : o0 + width],
-                                start=(g == 0),
-                                stop=(g == G - 1),
-                            )
-                    nc.vector.tensor_tensor(
-                        out=y[branch][:, bank_start : bank_start + BANK],
-                        in0=acc[:],
-                        in1=bias_rows[:, branch * C + bank_start : branch * C + bank_start + BANK],
-                        op=ADD,
-                    )
-                nc.sync.dma_start(out=outs[branch][b].rearrange("w h c -> (w h) c"), in_=y[branch][:])
-                if branch == BRANCH_ORDER[1]:
-                    first_two = results.tile([P, C], F32)
-                    nc.gpsimd.tensor_tensor(
-                        out=first_two[:], in0=y[BRANCH_ORDER[0]][:], in1=y[BRANCH_ORDER[1]][:], op=ADD
-                    )
-            return first_two, y[BRANCH_ORDER[2]]
+        def product(b, version, words, planes):
+            acc = banks.tile([P, BANK], F32)
+            for g in range(G):
+                nc.tensor.matmul_mx(
+                    out=acc[:],
+                    lhsT=x_words[version][:, b, g, :].bitcast(FP8X4),
+                    lhsT_scale=x_planes[version][:, b, g, :],
+                    rhs=words[g].bitcast(FP4X4),
+                    rhs_scale=planes[g],
+                    start=(g == 0),
+                    stop=(g == G - 1),
+                )
+            return acc
 
-        def sum_tokens(b, parts):
-            for i in range(0, BLOCKS, 2):
-                turned = turns.tile([P, 2, 2, P], F32)
-                for k in range(2):
-                    for n, part in enumerate(parts):
-                        nc.tensor.transpose(turned[:, k, n, :], part[:, (i + k) * P : (i + k + 1) * P], identity[:])
-                for k in range(2):
+        def project_batch(b):
+            rows = slice(b * T, (b + 1) * T)
+            y3 = results.tile([P, C], F32)
+            for c0 in range(0, C, BANK):
+                acc = product(
+                    b,
+                    SAME,
+                    [x3_words[:, g, 2 * c0 : 2 * (c0 + BANK)] for g in range(G)],
+                    [w_planes[:, g, 2 * C + c0 : 2 * C + c0 + BANK] for g in range(G)],
+                )
+                nc.vector.tensor_tensor(
+                    out=y3[:, c0 : c0 + BANK],
+                    in0=acc[:],
+                    in1=bias_rows[:, (2 * C + c0) // QUARTER : (2 * C + c0 + BANK) // QUARTER, :].rearrange("p q c -> p (q c)"),
+                    op=ADD,
+                )
+            nc.sync.dma_start(out=out_2.rearrange("b w h c -> (b w h) c")[rows, :], in_=y3[:])
+
+            y12 = results.tile([P, 8, QUARTER], F32)
+            z = sums.tile([P, C], F32)
+            for shift in SHIFTS:
+                acc = product(
+                    b,
+                    shift,
+                    [pair_words[:, g, shift].rearrange("p n k -> p (n k)") for g in range(G)],
+                    [pair_planes[:, g, shift].rearrange("p n c -> p (n c)") for g in range(G)],
+                )
+                second = 4 + x2_quarter(shift)
+                both = slice(shift, second + 1, second - shift)
+                nc.vector.tensor_tensor(
+                    out=y12[:, both, :],
+                    in0=acc[:].rearrange("p (n c) -> p n c", n=2),
+                    in1=bias_rows[:, both, :],
+                    op=ADD,
+                )
+            y1 = y12[:, 0:4, :].rearrange("p q c -> p (q c)")
+            y2 = y12[:, 4:8, :].rearrange("p q c -> p (q c)")
+            nc.sync.dma_start(out=out_0.rearrange("b w h c -> (b w h) c")[rows, :], in_=y1)
+            nc.sync.dma_start(out=out_1.rearrange("b w h c -> (b w h) c")[rows, :], in_=y2)
+            adder = nc.vector if b == B - 1 else nc.gpsimd
+            adder.tensor_tensor(out=z[:], in0=y3[:], in1=y1, op=ADD)
+            adder.tensor_tensor(out=z[:], in0=z[:], in1=y2, op=ADD)
+            return z
+
+        def sum_tokens(b, z):
+            for i in range(0, BLOCKS, 4):
+                turned = turns.tile([P, 4, P], F32)
+                for k in range(4):
+                    nc.tensor.transpose(turned[:, k, :], z[:, (i + k) * P : (i + k + 1) * P], identity[:])
+                for k in range(4):
                     nc.scalar.activation(
                         out=unread[:, i + k, :],
-                        in_=turned[:, k].rearrange("p n t -> p (n t)"),
+                        in_=turned[:, k, :],
                         func=COPY,
                         accum_out=a_by_channel[:, b * BLOCKS + i + k : b * BLOCKS + i + k + 1],
                     )
 
         ctx.enter_context(tc.manual_schedule())
-        for b in range(AHEAD):
-            quantise_batch(b)
-        parts_before = None
+        quantise_batch(0)
+        pair_scale_bytes()
+        quantise_batch(1)
+        z_of_batch = []
         for b in range(B):
+            z_of_batch.append(project_batch(b))
             if b + AHEAD < B:
                 quantise_batch(b + AHEAD)
-            parts = project_batch(b)
-            if parts_before is not None:
-                sum_tokens(b - 1, parts_before)
-            parts_before = parts
-        sum_tokens(B - 1, parts_before)
+            if b >= LATE:
+                sum_tokens(b - LATE, z_of_batch[b - LATE])
+        for b in range(B - LATE, B):
+            sum_tokens(b, z_of_batch[b])
 
         a_turned = turns.tile([P, P], F32, tag="turned")
         nc.tensor.transpose(a_turned[:], a_by_channel[:], identity[:])

@@ -24,7 +24,7 @@ BANK = 512
 BLOCKS = C // P
 TOKEN_WORDS = PACK // 2
 AHEAD = 2
-LATE = 2
+LATE = 1
 
 FLOPS = 2 * B * T * C * O
 
@@ -44,8 +44,8 @@ def tile_modelnew_pa_kernel(tc, x, w1_words, w1_scales, b1, out_0, out_1, out_2,
         stage = ctx.enter_context(tc.tile_pool(name="stage", bufs=3))
         results = ctx.enter_context(tc.tile_pool(name="results", bufs=3))
         sums = ctx.enter_context(tc.tile_pool(name="sums", bufs=LATE + 2))
-        banks = ctx.enter_context(tc.psum_pool(name="banks", bufs=6))
-        turns = ctx.enter_context(tc.psum_pool(name="turns", bufs=2))
+        banks = ctx.enter_context(tc.psum_pool(name="banks", bufs=4))
+        turns = ctx.enter_context(tc.psum_pool(name="turns", bufs=4))
 
         raw = keep.tile([P, B, G, PACK, T], BF16)
         w_planes = keep.tile([P, G, O], U8, align_bytes=64)
@@ -56,7 +56,7 @@ def tile_modelnew_pa_kernel(tc, x, w1_words, w1_scales, b1, out_0, out_1, out_2,
         x_words = [keep.tile([P, B, G, T], U32, align_bytes=64, name="x_words%d" % v) for v in range(5)]
         x_planes = [keep.tile([P, B, G, T], U8, align_bytes=64, name="x_planes%d" % v) for v in range(5)]
         identity = keep.tile([P, P], F32)
-        unread = keep.tile([P, BLOCKS, P], BF16)
+        unread = keep.tile([P, BLOCKS, 2 * P], BF16)
         a_by_channel = keep.tile([P, P], F32)
         a_rows = keep.tile([P, P], F32)
 
@@ -197,18 +197,18 @@ def tile_modelnew_pa_kernel(tc, x, w1_words, w1_scales, b1, out_0, out_1, out_2,
             nc.sync.dma_start(out=out_1.rearrange("b w h c -> (b w h) c")[rows, :], in_=y2)
             adder = nc.vector if b == B - 1 else nc.gpsimd
             adder.tensor_tensor(out=z[:], in0=y3[:], in1=y1, op=ADD)
-            adder.tensor_tensor(out=z[:], in0=z[:], in1=y2, op=ADD)
-            return z
+            return z[:], y2
 
-        def sum_tokens(b, z):
-            for i in range(0, BLOCKS, 4):
-                turned = turns.tile([P, 4, P], F32)
-                for k in range(4):
-                    nc.tensor.transpose(turned[:, k, :], z[:, (i + k) * P : (i + k + 1) * P], identity[:])
-                for k in range(4):
+        def sum_tokens(b, parts):
+            for i in range(0, BLOCKS, 2):
+                turned = turns.tile([P, 2, 2, P], F32)
+                for k in range(2):
+                    for n, part in enumerate(parts):
+                        nc.tensor.transpose(turned[:, k, n, :], part[:, (i + k) * P : (i + k + 1) * P], identity[:])
+                for k in range(2):
                     nc.scalar.activation(
                         out=unread[:, i + k, :],
-                        in_=turned[:, k, :],
+                        in_=turned[:, k].rearrange("p n t -> p (n t)"),
                         func=COPY,
                         accum_out=a_by_channel[:, b * BLOCKS + i + k : b * BLOCKS + i + k + 1],
                     )
@@ -217,15 +217,15 @@ def tile_modelnew_pa_kernel(tc, x, w1_words, w1_scales, b1, out_0, out_1, out_2,
         quantise_batch(0)
         pair_scale_bytes()
         quantise_batch(1)
-        z_of_batch = []
+        parts_of_batch = []
         for b in range(B):
-            z_of_batch.append(project_batch(b))
+            parts_of_batch.append(project_batch(b))
             if b + AHEAD < B:
                 quantise_batch(b + AHEAD)
             if b >= LATE:
-                sum_tokens(b - LATE, z_of_batch[b - LATE])
+                sum_tokens(b - LATE, parts_of_batch[b - LATE])
         for b in range(B - LATE, B):
-            sum_tokens(b, z_of_batch[b])
+            sum_tokens(b, parts_of_batch[b])
 
         a_turned = turns.tile([P, P], F32, tag="turned")
         nc.tensor.transpose(a_turned[:], a_by_channel[:], identity[:])

@@ -56,12 +56,16 @@ def tile_modelnew_pa_kernel(tc, x, w1_words, w1_scales, b1, out_0, out_1, out_2,
         x_words = [keep.tile([P, B, G, T], U32, align_bytes=64, name="x_words%d" % v) for v in range(5)]
         x_planes = [keep.tile([P, B, G, T], U8, align_bytes=64, name="x_planes%d" % v) for v in range(5)]
         identity = keep.tile([P, P], F32)
+        identity_bf16 = keep.tile([P, P], BF16)
+        bias_seed = keep.tile([P, BANK], BF16)
         unread = keep.tile([P, BLOCKS, 2 * P], BF16)
         a_by_channel = keep.tile([P, P], F32)
         a_rows = keep.tile([P, P], F32)
 
+        nc.vector.memset(bias_seed[:], 0.0)
         nc.vector.memset(w_planes[:].bitcast(I32), 0)
         nc.vector.memset(a_by_channel[:], 0.0)
+        make_identity(nc, identity_bf16[:])
         make_identity(nc, identity[:])
 
         def load_x(b):
@@ -70,6 +74,7 @@ def tile_modelnew_pa_kernel(tc, x, w1_words, w1_scales, b1, out_0, out_1, out_2,
                 in_=x[b].rearrange("(g p j) w h -> p g j (w h)", g=G, p=P, j=PACK),
             )
 
+        nc.sync.dma_start(out=bias_seed[0 : O // BANK, :], in_=b1.rearrange("(i n) -> i n", n=BANK))
         load_x(0)
         for r in range(4):
             nc.sync.dma_start(
@@ -80,7 +85,6 @@ def tile_modelnew_pa_kernel(tc, x, w1_words, w1_scales, b1, out_0, out_1, out_2,
             out=x3_words[:].bitcast(I32),
             in_=w1_words.rearrange("g p n -> p g n")[:, :, 4 * C : 6 * C].bitcast(I32),
         )
-        nc.sync.dma_start(out=bias_rows[:].rearrange("p q c -> p (q c)"), in_=b1.partition_broadcast(P))
         load_x(1)
         for g in range(G):
             nc.sync.dma_start(
@@ -95,6 +99,21 @@ def tile_modelnew_pa_kernel(tc, x, w1_words, w1_scales, b1, out_0, out_1, out_2,
                 )
         for b in range(2, B):
             load_x(b)
+
+        def spread_bias(branch):
+            spread = turns.tile([P, C], BF16, tag="turned")
+            for half in range(C // BANK):
+                i = branch * (C // BANK) + half
+                nc.tensor.matmul(
+                    out=spread[:, half * BANK : (half + 1) * BANK],
+                    lhsT=identity_bf16[:, i : i + 1].to_broadcast([P, P]),
+                    rhs=bias_seed[:],
+                    start=True,
+                    stop=True,
+                )
+            nc.vector.tensor_copy(
+                out=bias_rows[:, 4 * branch : 4 * branch + 4, :].rearrange("p q c -> p (q c)"), in_=spread[:]
+            )
 
         def pair_scale_bytes():
             nc.vector.tensor_copy(
@@ -214,7 +233,10 @@ def tile_modelnew_pa_kernel(tc, x, w1_words, w1_scales, b1, out_0, out_1, out_2,
                     )
 
         ctx.enter_context(tc.manual_schedule())
+        spread_bias(2)
         quantise_batch(0)
+        spread_bias(0)
+        spread_bias(1)
         pair_scale_bytes()
         quantise_batch(1)
         parts_of_batch = []

@@ -25,6 +25,7 @@ BLOCKS = C // P
 TOKEN_WORDS = PACK // 2
 AHEAD = 2
 LATE = 1
+QUANTISE_AFTER = 1
 
 FLOPS = 2 * B * T * C * O
 
@@ -53,8 +54,16 @@ def tile_modelnew_pa_kernel(tc, x, w1_words, w1_scales, b1, out_0, out_1, out_2,
         pair_words = keep.tile([P, G, 4, 2, 2 * QUARTER], U8, align_bytes=64)
         pair_planes = keep.tile([P, G, 4, 2, QUARTER], U8, align_bytes=64)
         bias_rows = keep.tile([P, O // QUARTER, QUARTER], BF16)
-        x_words = [keep.tile([P, B, G, T], U32, align_bytes=64, name="x_words%d" % v) for v in range(5)]
+        row_words = keep.tile([P, B, G, T + 2 * H], U32, align_bytes=64)
+        h_words = {v: keep.tile([P, B, G, T], U32, align_bytes=64, name="h_words%d" % v) for v in (H_MINUS, H_PLUS)}
         x_planes = [keep.tile([P, B, G, T], U8, align_bytes=64, name="x_planes%d" % v) for v in range(5)]
+        window_start = {W_MINUS: 0, SAME: H, W_PLUS: 2 * H}
+
+        def x_words(version, b, g):
+            if version in window_start:
+                return row_words[:, b, g, window_start[version] : window_start[version] + T]
+            return h_words[version][:, b, g, :]
+
         identity = keep.tile([P, P], F32)
         identity_bf16 = keep.tile([P, P], BF16)
         bias_seed = keep.tile([P, BANK], BF16)
@@ -128,26 +137,17 @@ def tile_modelnew_pa_kernel(tc, x, w1_words, w1_scales, b1, out_0, out_1, out_2,
                 )
 
         def quantise_batch(b):
-            padded = stage.tile([P, G, T + 2 * H, PACK], BF16, align_bytes=64)
-            by_token = raw[:, b].rearrange("p g j t -> p g t j")
-            nc.scalar.copy(out=padded[:, :, H : H + T, :], in_=by_token)
-            nc.scalar.copy(out=padded[:, :, 0:H, :], in_=by_token[:, :, 0:H, :])
-            nc.scalar.copy(out=padded[:, :, H + T : 2 * H + T, :], in_=by_token[:, :, T - H : T, :])
-            for version, start in ((SAME, H), (W_MINUS, 0), (W_PLUS, 2 * H)):
-                for g in range(G):
-                    nc.vector.quantize_mx(
-                        out=x_words[version][:, b, g, :].bitcast(FP8X4),
-                        scales=x_planes[version][:, b, g, :],
-                        in_=padded[:, g, start : start + T, :].rearrange("p t j -> p (t j)"),
-                    )
+            grouped = stage.tile([P, G, T, PACK], BF16, align_bytes=64)
+            nc.scalar.copy(out=grouped[:], in_=raw[:, b].rearrange("p g j t -> p g t j"))
+            for g in range(G):
+                nc.vector.quantize_mx(
+                    out=x_words(SAME, b, g).bitcast(FP8X4),
+                    scales=x_planes[SAME][:, b, g, :],
+                    in_=grouped[:, g].rearrange("p t j -> p (t j)"),
+                )
             row = TOKEN_WORDS * H
             last = row - TOKEN_WORDS
-            grid = (
-                padded[:, :, H : H + T, :]
-                .rearrange("p g t j -> p g (t j)")
-                .bitcast(F32)
-                .rearrange("p g (w k) -> p g w k", k=row)
-            )
+            grid = grouped[:].rearrange("p g t j -> p g (t j)").bitcast(F32).rearrange("p g (w k) -> p g w k", k=row)
             h_minus = stage.tile([P, G, W, H * PACK], BF16, align_bytes=64)
             nc.scalar.copy(out=h_minus[:].bitcast(F32)[:, :, :, TOKEN_WORDS:row], in_=grid[:, :, :, 0:last])
             nc.scalar.copy(out=h_minus[:].bitcast(F32)[:, :, :, 0:TOKEN_WORDS], in_=grid[:, :, :, 0:TOKEN_WORDS])
@@ -156,17 +156,26 @@ def tile_modelnew_pa_kernel(tc, x, w1_words, w1_scales, b1, out_0, out_1, out_2,
             nc.scalar.copy(out=h_plus[:].bitcast(F32)[:, :, :, last:row], in_=grid[:, :, :, last:row])
             for version, shifted in ((H_MINUS, h_minus), (H_PLUS, h_plus)):
                 nc.vector.quantize_mx(
-                    out=x_words[version][:, b].rearrange("p g t -> p (g t)").bitcast(FP8X4),
+                    out=h_words[version][:, b].rearrange("p g t -> p (g t)").bitcast(FP8X4),
                     scales=x_planes[version][:, b].rearrange("p g t -> p (g t)"),
                     in_=shifted[:].rearrange("p g w k -> p (g w k)"),
                 )
+            rows = row_words[:, b].bitcast(I32).rearrange("p g (w h) -> p g w h", h=H)
+            nc.vector.tensor_copy(out=rows[:, :, 0 : W + 2 : W + 1, :], in_=rows[:, :, 1 : W + 1 : W - 1, :])
+            same, down, up = (
+                x_planes[v][:, b].bitcast(I32).rearrange("p g (w k) -> p g w k", w=W) for v in (SAME, W_MINUS, W_PLUS)
+            )
+            nc.vector.tensor_copy(out=down[:, :, 1:W, :], in_=same[:, :, 0 : W - 1, :])
+            nc.vector.tensor_copy(out=down[:, :, 0:1, :], in_=same[:, :, 0:1, :])
+            nc.vector.tensor_copy(out=up[:, :, 0 : W - 1, :], in_=same[:, :, 1:W, :])
+            nc.vector.tensor_copy(out=up[:, :, W - 1 : W, :], in_=same[:, :, W - 1 : W, :])
 
         def product(b, version, words, planes):
             acc = banks.tile([P, BANK], F32)
             for g in range(G):
                 nc.tensor.matmul_mx(
                     out=acc[:],
-                    lhsT=x_words[version][:, b, g, :].bitcast(FP8X4),
+                    lhsT=x_words(version, b, g).bitcast(FP8X4),
                     lhsT_scale=x_planes[version][:, b, g, :],
                     rhs=words[g].bitcast(FP4X4),
                     rhs_scale=planes[g],
@@ -210,27 +219,28 @@ def tile_modelnew_pa_kernel(tc, x, w1_words, w1_scales, b1, out_0, out_1, out_2,
                     in1=bias_rows[:, both, :],
                     op=ADD,
                 )
+                if shift == QUANTISE_AFTER and b + AHEAD < B:
+                    quantise_batch(b + AHEAD)
             y1 = y12[:, 0:4, :].rearrange("p q c -> p (q c)")
             y2 = y12[:, 4:8, :].rearrange("p q c -> p (q c)")
             nc.sync.dma_start(out=out_0.rearrange("b w h c -> (b w h) c")[rows, :], in_=y1)
             nc.sync.dma_start(out=out_1.rearrange("b w h c -> (b w h) c")[rows, :], in_=y2)
             adder = nc.vector if b == B - 1 else nc.gpsimd
             adder.tensor_tensor(out=z[:], in0=y3[:], in1=y1, op=ADD)
-            return z[:], y2
+            return y2, z[:]
 
         def sum_tokens(b, parts):
-            for i in range(0, BLOCKS, 2):
-                turned = turns.tile([P, 2, 2, P], F32)
-                for k in range(2):
-                    for n, part in enumerate(parts):
-                        nc.tensor.transpose(turned[:, k, n, :], part[:, (i + k) * P : (i + k + 1) * P], identity[:])
-                for k in range(2):
-                    nc.scalar.activation(
-                        out=unread[:, i + k, :],
-                        in_=turned[:, k].rearrange("p n t -> p (n t)"),
-                        func=COPY,
-                        accum_out=a_by_channel[:, b * BLOCKS + i + k : b * BLOCKS + i + k + 1],
-                    )
+            turned = [turns.tile([P, 2, 2, P], F32, name="turned") for pair in range(BLOCKS // 2)]
+            for n, part in enumerate(parts):
+                for i in range(BLOCKS):
+                    nc.tensor.transpose(turned[i // 2][:, i % 2, n, :], part[:, i * P : (i + 1) * P], identity[:])
+            for i in range(BLOCKS):
+                nc.scalar.activation(
+                    out=unread[:, i, :],
+                    in_=turned[i // 2][:, i % 2].rearrange("p n t -> p (n t)"),
+                    func=COPY,
+                    accum_out=a_by_channel[:, b * BLOCKS + i : b * BLOCKS + i + 1],
+                )
 
         ctx.enter_context(tc.manual_schedule())
         spread_bias(2)
@@ -242,8 +252,6 @@ def tile_modelnew_pa_kernel(tc, x, w1_words, w1_scales, b1, out_0, out_1, out_2,
         parts_of_batch = []
         for b in range(B):
             parts_of_batch.append(project_batch(b))
-            if b + AHEAD < B:
-                quantise_batch(b + AHEAD)
             if b >= LATE:
                 sum_tokens(b - LATE, parts_of_batch[b - LATE])
         for b in range(B - LATE, B):

@@ -136,15 +136,9 @@ def tile_modelnew_pa_kernel(tc, x, w1_words, w1_scales, b1, out_0, out_1, out_2,
                     in_=w_planes[:, :, first : first + 2 * QUARTER].rearrange("p g (s c) -> p g s c", s=2).bitcast(I32),
                 )
 
-        def quantise_batch(b):
+        def stage_batch(b):
             grouped = stage.tile([P, G, T, PACK], BF16, align_bytes=64)
             nc.scalar.copy(out=grouped[:], in_=raw[:, b].rearrange("p g j t -> p g t j"))
-            for g in range(G):
-                nc.vector.quantize_mx(
-                    out=x_words(SAME, b, g).bitcast(FP8X4),
-                    scales=x_planes[SAME][:, b, g, :],
-                    in_=grouped[:, g].rearrange("p t j -> p (t j)"),
-                )
             row = TOKEN_WORDS * H
             last = row - TOKEN_WORDS
             grid = grouped[:].rearrange("p g t j -> p g (t j)").bitcast(F32).rearrange("p g (w k) -> p g w k", k=row)
@@ -154,6 +148,15 @@ def tile_modelnew_pa_kernel(tc, x, w1_words, w1_scales, b1, out_0, out_1, out_2,
             h_plus = stage.tile([P, G, W, H * PACK], BF16, align_bytes=64)
             nc.scalar.copy(out=h_plus[:].bitcast(F32)[:, :, :, 0:last], in_=grid[:, :, :, TOKEN_WORDS:row])
             nc.scalar.copy(out=h_plus[:].bitcast(F32)[:, :, :, last:row], in_=grid[:, :, :, last:row])
+            return grouped, h_minus, h_plus
+
+        def quantise_batch(b, grouped, h_minus, h_plus):
+            for g in range(G):
+                nc.vector.quantize_mx(
+                    out=x_words(SAME, b, g).bitcast(FP8X4),
+                    scales=x_planes[SAME][:, b, g, :],
+                    in_=grouped[:, g].rearrange("p t j -> p (t j)"),
+                )
             for version, shifted in ((H_MINUS, h_minus), (H_PLUS, h_plus)):
                 nc.vector.quantize_mx(
                     out=h_words[version][:, b].rearrange("p g t -> p (g t)").bitcast(FP8X4),
@@ -220,7 +223,9 @@ def tile_modelnew_pa_kernel(tc, x, w1_words, w1_scales, b1, out_0, out_1, out_2,
                     op=ADD,
                 )
                 if shift == QUANTISE_AFTER and b + AHEAD < B:
-                    quantise_batch(b + AHEAD)
+                    quantise_batch(b + AHEAD, *staged[b + AHEAD])
+                    if b + AHEAD + 1 < B:
+                        staged[b + AHEAD + 1] = stage_batch(b + AHEAD + 1)
             y1 = y12[:, 0:4, :].rearrange("p q c -> p (q c)")
             y2 = y12[:, 4:8, :].rearrange("p q c -> p (q c)")
             nc.sync.dma_start(out=out_0.rearrange("b w h c -> (b w h) c")[rows, :], in_=y1)
@@ -243,12 +248,16 @@ def tile_modelnew_pa_kernel(tc, x, w1_words, w1_scales, b1, out_0, out_1, out_2,
                 )
 
         ctx.enter_context(tc.manual_schedule())
+        staged = {}
         spread_bias(2)
-        quantise_batch(0)
+        staged[0] = stage_batch(0)
+        quantise_batch(0, *staged[0])
         spread_bias(0)
         spread_bias(1)
         pair_scale_bytes()
-        quantise_batch(1)
+        staged[1] = stage_batch(1)
+        quantise_batch(1, *staged[1])
+        staged[2] = stage_batch(2)
         parts_of_batch = []
         for b in range(B):
             parts_of_batch.append(project_batch(b))

@@ -23,7 +23,7 @@ QUARTER = C // 4
 BANK = 512
 BLOCKS = C // P
 TOKEN_WORDS = PACK // 2
-AHEAD = 2
+AHEAD = 1
 LATE = 1
 QUANTISE_AFTER = 1
 
@@ -83,29 +83,32 @@ def tile_modelnew_pa_kernel(tc, x, w1_words, w1_scales, b1, out_0, out_1, out_2,
                 in_=x[b].rearrange("(g p j) w h -> p g j (w h)", g=G, p=P, j=PACK),
             )
 
-        nc.sync.dma_start(out=bias_seed[0 : O // BANK, :], in_=b1.rearrange("(i n) -> i n", n=BANK))
+        def load_pair_words(first_shift):
+            shifts = slice(first_shift, first_shift + 2)
+            for g in range(G):
+                for branch, first_quarter in ((0, first_shift), (1, 4 + x2_quarter(first_shift))):
+                    first = 2 * first_quarter * QUARTER
+                    nc.sync.dma_start(
+                        out=pair_words[:, g, shifts, branch, :].bitcast(I32),
+                        in_=w1_words[g, :, first : first + 4 * QUARTER].rearrange("p (s k) -> p s k", s=2).bitcast(I32),
+                    )
+
         load_x(0)
+        nc.sync.dma_start(
+            out=x3_words[:].bitcast(I32),
+            in_=w1_words.rearrange("g p n -> p g n")[:, :, 4 * C : 6 * C].bitcast(I32),
+        )
+        bias_by_row = b1.rearrange("(i n) -> i n", n=BANK)
+        nc.sync.dma_start(out=bias_seed[4:6, :], in_=bias_by_row[4:6, :])
+        nc.sync.dma_start(out=bias_seed[0:4, :], in_=bias_by_row[0:4, :])
         for r in range(4):
             nc.sync.dma_start(
                 out=w_planes[r : P : 32, :, :].bitcast(I32),
                 in_=w1_scales[:, r : 16 : 4, :].rearrange("g q n -> q g n").bitcast(I32),
             )
-        nc.sync.dma_start(
-            out=x3_words[:].bitcast(I32),
-            in_=w1_words.rearrange("g p n -> p g n")[:, :, 4 * C : 6 * C].bitcast(I32),
-        )
+        load_pair_words(0)
         load_x(1)
-        for g in range(G):
-            nc.sync.dma_start(
-                out=pair_words[:, g, :, 0, :].bitcast(I32),
-                in_=w1_words[g, :, 0 : 2 * C].rearrange("p (s k) -> p s k", s=4).bitcast(I32),
-            )
-            for shift in (0, 2):
-                first = 2 * (C + x2_quarter(shift) * QUARTER)
-                nc.sync.dma_start(
-                    out=pair_words[:, g, shift : shift + 2, 1, :].bitcast(I32),
-                    in_=w1_words[g, :, first : first + 4 * QUARTER].rearrange("p (s k) -> p s k", s=2).bitcast(I32),
-                )
+        load_pair_words(2)
         for b in range(2, B):
             load_x(b)
 
@@ -138,7 +141,8 @@ def tile_modelnew_pa_kernel(tc, x, w1_words, w1_scales, b1, out_0, out_1, out_2,
 
         def stage_batch(b):
             grouped = stage.tile([P, G, T, PACK], BF16, align_bytes=64)
-            nc.scalar.copy(out=grouped[:], in_=raw[:, b].rearrange("p g j t -> p g t j"))
+            interleave = nc.vector.tensor_copy if b == 0 else nc.scalar.copy
+            interleave(out=grouped[:], in_=raw[:, b].rearrange("p g j t -> p g t j"))
             row = TOKEN_WORDS * H
             last = row - TOKEN_WORDS
             grid = grouped[:].rearrange("p g t j -> p g (t j)").bitcast(F32).rearrange("p g (w k) -> p g w k", k=row)
@@ -150,19 +154,23 @@ def tile_modelnew_pa_kernel(tc, x, w1_words, w1_scales, b1, out_0, out_1, out_2,
             nc.scalar.copy(out=h_plus[:].bitcast(F32)[:, :, :, last:row], in_=grid[:, :, :, last:row])
             return grouped, h_minus, h_plus
 
-        def quantise_batch(b, grouped, h_minus, h_plus):
+        def quantise_same(b, grouped):
             for g in range(G):
                 nc.vector.quantize_mx(
                     out=x_words(SAME, b, g).bitcast(FP8X4),
                     scales=x_planes[SAME][:, b, g, :],
                     in_=grouped[:, g].rearrange("p t j -> p (t j)"),
                 )
+
+        def quantise_shifted(b, h_minus, h_plus):
             for version, shifted in ((H_MINUS, h_minus), (H_PLUS, h_plus)):
                 nc.vector.quantize_mx(
                     out=h_words[version][:, b].rearrange("p g t -> p (g t)").bitcast(FP8X4),
                     scales=x_planes[version][:, b].rearrange("p g t -> p (g t)"),
                     in_=shifted[:].rearrange("p g w k -> p (g w k)"),
                 )
+
+        def move_rows(b):
             rows = row_words[:, b].bitcast(I32).rearrange("p g (w h) -> p g w h", h=H)
             nc.vector.tensor_copy(out=rows[:, :, 0 : W + 2 : W + 1, :], in_=rows[:, :, 1 : W + 1 : W - 1, :])
             same, down, up = (
@@ -204,6 +212,9 @@ def tile_modelnew_pa_kernel(tc, x, w1_words, w1_scales, b1, out_0, out_1, out_2,
                     op=ADD,
                 )
             nc.sync.dma_start(out=out_2.rearrange("b w h c -> (b w h) c")[rows, :], in_=y3[:])
+            if b == 0:
+                spread_bias(0)
+                spread_bias(1)
 
             y12 = results.tile([P, 8, QUARTER], F32)
             z = sums.tile([P, C], F32)
@@ -223,7 +234,10 @@ def tile_modelnew_pa_kernel(tc, x, w1_words, w1_scales, b1, out_0, out_1, out_2,
                     op=ADD,
                 )
                 if shift == QUANTISE_AFTER and b + AHEAD < B:
-                    quantise_batch(b + AHEAD, *staged[b + AHEAD])
+                    grouped, h_minus, h_plus = staged[b + AHEAD]
+                    quantise_same(b + AHEAD, grouped)
+                    quantise_shifted(b + AHEAD, h_minus, h_plus)
+                    move_rows(b + AHEAD)
                     if b + AHEAD + 1 < B:
                         staged[b + AHEAD + 1] = stage_batch(b + AHEAD + 1)
             y1 = y12[:, 0:4, :].rearrange("p q c -> p (q c)")
@@ -239,25 +253,31 @@ def tile_modelnew_pa_kernel(tc, x, w1_words, w1_scales, b1, out_0, out_1, out_2,
             for n, part in enumerate(parts):
                 for i in range(BLOCKS):
                     nc.tensor.transpose(turned[i // 2][:, i % 2, n, :], part[:, i * P : (i + 1) * P], identity[:])
-            for i in range(BLOCKS):
+            scalar_blocks = BLOCKS if b < B - 1 - LATE else BLOCKS // 2
+            for i in range(scalar_blocks):
                 nc.scalar.activation(
                     out=unread[:, i, :],
                     in_=turned[i // 2][:, i % 2].rearrange("p n t -> p (n t)"),
                     func=COPY,
                     accum_out=a_by_channel[:, b * BLOCKS + i : b * BLOCKS + i + 1],
                 )
+            for i in range(scalar_blocks, BLOCKS, 2):
+                nc.vector.tensor_reduce(
+                    out=a_by_channel[:, b * BLOCKS + i : b * BLOCKS + i + 2],
+                    in_=turned[i // 2][:].rearrange("p i n t -> p i (n t)"),
+                    op=ADD,
+                    axis=mybir.AxisListType.X,
+                )
 
         ctx.enter_context(tc.manual_schedule())
         staged = {}
-        spread_bias(2)
         staged[0] = stage_batch(0)
-        quantise_batch(0, *staged[0])
-        spread_bias(0)
-        spread_bias(1)
+        quantise_same(0, staged[0][0])
+        spread_bias(2)
         pair_scale_bytes()
+        move_rows(0)
+        quantise_shifted(0, staged[0][1], staged[0][2])
         staged[1] = stage_batch(1)
-        quantise_batch(1, *staged[1])
-        staged[2] = stage_batch(2)
         parts_of_batch = []
         for b in range(B):
             parts_of_batch.append(project_batch(b))

@@ -33,6 +33,9 @@ W_MINUS, W_PLUS, H_MINUS, H_PLUS, SAME = range(5)
 SHIFTS = (W_MINUS, W_PLUS, H_MINUS, H_PLUS)
 
 
+QUARTER_ORDER = (0, 2, 1, 3)
+
+
 def x2_quarter(shift):
     return (shift + 2) % 4
 
@@ -71,7 +74,7 @@ def tile_modelnew_pa_kernel(tc, x, w1_words, w1_scales, b1, out_0, out_1, out_2,
         a_by_channel = keep.tile([P, P], F32)
         a_rows = keep.tile([P, P], F32)
 
-        nc.vector.memset(bias_seed[:], 0.0)
+        nc.gpsimd.memset(bias_seed[:], 0.0)
         nc.vector.memset(w_planes[:].bitcast(I32), 0)
         nc.vector.memset(a_by_channel[:], 0.0)
         make_identity(nc, identity_bf16[:])
@@ -94,13 +97,13 @@ def tile_modelnew_pa_kernel(tc, x, w1_words, w1_scales, b1, out_0, out_1, out_2,
                     )
 
         load_x(0)
+        bias_by_row = b1.rearrange("(i n) -> i n", n=BANK)
+        nc.sync.dma_start(out=bias_seed[4:6, :], in_=bias_by_row[4:6, :])
+        nc.sync.dma_start(out=bias_seed[0:4, :], in_=bias_by_row[0:4, :])
         nc.sync.dma_start(
             out=x3_words[:].bitcast(I32),
             in_=w1_words.rearrange("g p n -> p g n")[:, :, 4 * C : 6 * C].bitcast(I32),
         )
-        bias_by_row = b1.rearrange("(i n) -> i n", n=BANK)
-        nc.sync.dma_start(out=bias_seed[4:6, :], in_=bias_by_row[4:6, :])
-        nc.sync.dma_start(out=bias_seed[0:4, :], in_=bias_by_row[0:4, :])
         for r in range(4):
             nc.sync.dma_start(
                 out=w_planes[r : P : 32, :, :].bitcast(I32),
@@ -123,6 +126,9 @@ def tile_modelnew_pa_kernel(tc, x, w1_words, w1_scales, b1, out_0, out_1, out_2,
                     start=True,
                     stop=True,
                 )
+            return spread
+
+        def keep_bias(branch, spread):
             nc.vector.tensor_copy(
                 out=bias_rows[:, 4 * branch : 4 * branch + 4, :].rearrange("p q c -> p (q c)"), in_=spread[:]
             )
@@ -212,9 +218,6 @@ def tile_modelnew_pa_kernel(tc, x, w1_words, w1_scales, b1, out_0, out_1, out_2,
                     op=ADD,
                 )
             nc.sync.dma_start(out=out_2.rearrange("b w h c -> (b w h) c")[rows, :], in_=y3[:])
-            if b == 0:
-                spread_bias(0)
-                spread_bias(1)
 
             y12 = results.tile([P, 8, QUARTER], F32)
             z = sums.tile([P, C], F32)
@@ -233,6 +236,9 @@ def tile_modelnew_pa_kernel(tc, x, w1_words, w1_scales, b1, out_0, out_1, out_2,
                     in1=bias_rows[:, both, :],
                     op=ADD,
                 )
+                if b == B - 1:
+                    quarter = slice(shift * QUARTER, (shift + 1) * QUARTER)
+                    nc.vector.tensor_tensor(out=z[:, quarter], in0=y3[:, quarter], in1=y12[:, shift, :], op=ADD)
                 if shift == QUANTISE_AFTER and b + AHEAD < B:
                     grouped, h_minus, h_plus = staged[b + AHEAD]
                     quantise_same(b + AHEAD, grouped)
@@ -244,39 +250,51 @@ def tile_modelnew_pa_kernel(tc, x, w1_words, w1_scales, b1, out_0, out_1, out_2,
             y2 = y12[:, 4:8, :].rearrange("p q c -> p (q c)")
             nc.sync.dma_start(out=out_0.rearrange("b w h c -> (b w h) c")[rows, :], in_=y1)
             nc.sync.dma_start(out=out_1.rearrange("b w h c -> (b w h) c")[rows, :], in_=y2)
-            adder = nc.vector if b == B - 1 else nc.gpsimd
-            adder.tensor_tensor(out=z[:], in0=y3[:], in1=y1, op=ADD)
+            if b < B - 1:
+                nc.gpsimd.tensor_tensor(out=z[:], in0=y3[:], in1=y1, op=ADD)
             return y2, z[:]
 
         def sum_tokens(b, parts):
-            turned = [turns.tile([P, 2, 2, P], F32, name="turned") for pair in range(BLOCKS // 2)]
-            for n, part in enumerate(parts):
-                for i in range(BLOCKS):
-                    nc.tensor.transpose(turned[i // 2][:, i % 2, n, :], part[:, i * P : (i + 1) * P], identity[:])
-            scalar_blocks = BLOCKS if b < B - 1 - LATE else BLOCKS // 2
-            for i in range(scalar_blocks):
-                nc.scalar.activation(
-                    out=unread[:, i, :],
-                    in_=turned[i // 2][:, i % 2].rearrange("p n t -> p (n t)"),
-                    func=COPY,
-                    accum_out=a_by_channel[:, b * BLOCKS + i : b * BLOCKS + i + 1],
-                )
-            for i in range(scalar_blocks, BLOCKS, 2):
-                nc.vector.tensor_reduce(
-                    out=a_by_channel[:, b * BLOCKS + i : b * BLOCKS + i + 2],
-                    in_=turned[i // 2][:].rearrange("p i n t -> p i (n t)"),
-                    op=ADD,
-                    axis=mybir.AxisListType.X,
-                )
+            if b < B - 1:
+                turned = [turns.tile([P, 2, 2, P], F32, name="turned") for quarter in range(4)]
+                order = [(n, i) for n in range(2) for i in range(BLOCKS)]
+                quarters = range(4)
+            else:
+                turned = [banks.tile([P, 2, 2, P], F32, name="acc") for quarter in range(4)]
+                order = [(n, 2 * quarter + i) for quarter in QUARTER_ORDER for n in range(2) for i in range(2)]
+                quarters = QUARTER_ORDER
+            for n, i in order:
+                nc.tensor.transpose(turned[i // 2][:, i % 2, n, :], parts[n][:, i * P : (i + 1) * P], identity[:])
+            vector_quarters = (2, 3) if b >= B - 1 - LATE else ()
+            for quarter in quarters:
+                first = b * BLOCKS + 2 * quarter
+                if quarter in vector_quarters:
+                    nc.vector.tensor_reduce(
+                        out=a_by_channel[:, first : first + 2],
+                        in_=turned[quarter][:].rearrange("p i n t -> p i (n t)"),
+                        op=ADD,
+                        axis=mybir.AxisListType.X,
+                    )
+                    continue
+                for i in range(2):
+                    nc.scalar.activation(
+                        out=unread[:, 2 * quarter + i, :],
+                        in_=turned[quarter][:, i].rearrange("p n t -> p (n t)"),
+                        func=COPY,
+                        accum_out=a_by_channel[:, first + i : first + i + 1],
+                    )
 
         ctx.enter_context(tc.manual_schedule())
         staged = {}
+        spread = {branch: spread_bias(branch) for branch in (2, 0, 1)}
         staged[0] = stage_batch(0)
         quantise_same(0, staged[0][0])
-        spread_bias(2)
+        keep_bias(2, spread[2])
         pair_scale_bytes()
         move_rows(0)
         quantise_shifted(0, staged[0][1], staged[0][2])
+        keep_bias(0, spread[0])
+        keep_bias(1, spread[1])
         staged[1] = stage_batch(1)
         parts_of_batch = []
         for b in range(B):

@@ -25,7 +25,7 @@ BLOCKS = C // P
 TOKEN_WORDS = PACK // 2
 AHEAD = 1
 LATE = 1
-QUANTISE_AFTER = 1
+QUANTISE_AFTER = 2
 
 FLOPS = 2 * B * T * C * O
 
@@ -128,10 +128,8 @@ def tile_modelnew_pa_kernel(tc, x, w1_words, w1_scales, b1, out_0, out_1, out_2,
                 )
             return spread
 
-        def keep_bias(branch, spread):
-            nc.vector.tensor_copy(
-                out=bias_rows[:, 4 * branch : 4 * branch + 4, :].rearrange("p q c -> p (q c)"), in_=spread[:]
-            )
+        def keep_bias(branch, spread, copy):
+            copy(out=bias_rows[:, 4 * branch : 4 * branch + 4, :].rearrange("p q c -> p (q c)"), in_=spread[:])
 
         def pair_scale_bytes():
             nc.vector.tensor_copy(
@@ -289,12 +287,12 @@ def tile_modelnew_pa_kernel(tc, x, w1_words, w1_scales, b1, out_0, out_1, out_2,
         spread = {branch: spread_bias(branch) for branch in (2, 0, 1)}
         staged[0] = stage_batch(0)
         quantise_same(0, staged[0][0])
-        keep_bias(2, spread[2])
+        keep_bias(2, spread[2], nc.vector.tensor_copy)
         pair_scale_bytes()
         move_rows(0)
         quantise_shifted(0, staged[0][1], staged[0][2])
-        keep_bias(0, spread[0])
-        keep_bias(1, spread[1])
+        keep_bias(0, spread[0], nc.scalar.copy)
+        keep_bias(1, spread[1], nc.scalar.copy)
         staged[1] = stage_batch(1)
         parts_of_batch = []
         for b in range(B):

@@ -58,14 +58,23 @@ def tile_modelnew_pa_kernel(tc, x, w1_words, w1_scales, b1, out_0, out_1, out_2,
         pair_planes = keep.tile([P, G, 4, 2, QUARTER], U8, align_bytes=64)
         bias_rows = keep.tile([P, O // QUARTER, QUARTER], BF16)
         row_words = keep.tile([P, B, G, T + 2 * H], U32, align_bytes=64)
-        h_words = {v: keep.tile([P, B, G, T], U32, align_bytes=64, name="h_words%d" % v) for v in (H_MINUS, H_PLUS)}
-        x_planes = [keep.tile([P, B, G, T], U8, align_bytes=64, name="x_planes%d" % v) for v in range(5)]
+        h_words = keep.tile([P, B, 2, G, T], U32, align_bytes=64)
+        same_planes = keep.tile([P, B, G, T], U8, align_bytes=64)
+        w_shift_planes = keep.tile([P, B, G, 2, T], U8, align_bytes=64)
+        h_planes = keep.tile([P, B, 2, G, T], U8, align_bytes=64)
         window_start = {W_MINUS: 0, SAME: H, W_PLUS: 2 * H}
 
         def x_words(version, b, g):
             if version in window_start:
                 return row_words[:, b, g, window_start[version] : window_start[version] + T]
-            return h_words[version][:, b, g, :]
+            return h_words[:, b, version - H_MINUS, g, :]
+
+        def x_scales(version, b, g):
+            if version == SAME:
+                return same_planes[:, b, g, :]
+            if version in window_start:
+                return w_shift_planes[:, b, g, version - W_MINUS, :]
+            return h_planes[:, b, version - H_MINUS, g, :]
 
         identity = keep.tile([P, P], F32)
         identity_bf16 = keep.tile([P, P], BF16)
@@ -76,7 +85,7 @@ def tile_modelnew_pa_kernel(tc, x, w1_words, w1_scales, b1, out_0, out_1, out_2,
 
         nc.gpsimd.memset(bias_seed[:], 0.0)
         nc.vector.memset(w_planes[:].bitcast(I32), 0)
-        nc.vector.memset(a_by_channel[:], 0.0)
+        nc.gpsimd.memset(a_by_channel[:], 0.0)
         make_identity(nc, identity_bf16[:])
         make_identity(nc, identity[:])
 
@@ -143,47 +152,52 @@ def tile_modelnew_pa_kernel(tc, x, w1_words, w1_scales, b1, out_0, out_1, out_2,
                     in_=w_planes[:, :, first : first + 2 * QUARTER].rearrange("p g (s c) -> p g s c", s=2).bitcast(I32),
                 )
 
-        def stage_batch(b):
+        def interleave(b):
             grouped = stage.tile([P, G, T, PACK], BF16, align_bytes=64)
-            interleave = nc.vector.tensor_copy if b == 0 else nc.scalar.copy
-            interleave(out=grouped[:], in_=raw[:, b].rearrange("p g j t -> p g t j"))
+            copy = nc.vector.tensor_copy if b == 0 else nc.scalar.copy
+            copy(out=grouped[:], in_=raw[:, b].rearrange("p g j t -> p g t j"))
+            return grouped
+
+        def shift_in_h(grouped):
             row = TOKEN_WORDS * H
             last = row - TOKEN_WORDS
             grid = grouped[:].rearrange("p g t j -> p g (t j)").bitcast(F32).rearrange("p g (w k) -> p g w k", k=row)
-            h_minus = stage.tile([P, G, W, H * PACK], BF16, align_bytes=64)
-            nc.scalar.copy(out=h_minus[:].bitcast(F32)[:, :, :, TOKEN_WORDS:row], in_=grid[:, :, :, 0:last])
-            nc.scalar.copy(out=h_minus[:].bitcast(F32)[:, :, :, 0:TOKEN_WORDS], in_=grid[:, :, :, 0:TOKEN_WORDS])
-            h_plus = stage.tile([P, G, W, H * PACK], BF16, align_bytes=64)
-            nc.scalar.copy(out=h_plus[:].bitcast(F32)[:, :, :, 0:last], in_=grid[:, :, :, TOKEN_WORDS:row])
-            nc.scalar.copy(out=h_plus[:].bitcast(F32)[:, :, :, last:row], in_=grid[:, :, :, last:row])
-            return grouped, h_minus, h_plus
+            shifted = stage.tile([P, 2, G, W, H * PACK], BF16, align_bytes=64)
+            h_minus = shifted[:, 0].bitcast(F32)
+            h_plus = shifted[:, 1].bitcast(F32)
+            nc.scalar.copy(out=h_minus[:, :, :, TOKEN_WORDS:row], in_=grid[:, :, :, 0:last])
+            nc.scalar.copy(out=h_minus[:, :, :, 0:TOKEN_WORDS], in_=grid[:, :, :, 0:TOKEN_WORDS])
+            nc.scalar.copy(out=h_plus[:, :, :, 0:last], in_=grid[:, :, :, TOKEN_WORDS:row])
+            nc.scalar.copy(out=h_plus[:, :, :, last:row], in_=grid[:, :, :, last:row])
+            return shifted
+
+        def stage_batch(b):
+            grouped = interleave(b)
+            return grouped, shift_in_h(grouped)
 
         def quantise_same(b, grouped):
             for g in range(G):
                 nc.vector.quantize_mx(
                     out=x_words(SAME, b, g).bitcast(FP8X4),
-                    scales=x_planes[SAME][:, b, g, :],
+                    scales=x_scales(SAME, b, g),
                     in_=grouped[:, g].rearrange("p t j -> p (t j)"),
                 )
 
-        def quantise_shifted(b, h_minus, h_plus):
-            for version, shifted in ((H_MINUS, h_minus), (H_PLUS, h_plus)):
-                nc.vector.quantize_mx(
-                    out=h_words[version][:, b].rearrange("p g t -> p (g t)").bitcast(FP8X4),
-                    scales=x_planes[version][:, b].rearrange("p g t -> p (g t)"),
-                    in_=shifted[:].rearrange("p g w k -> p (g w k)"),
-                )
+        def quantise_shifted(b, shifted):
+            nc.vector.quantize_mx(
+                out=h_words[:, b].rearrange("p v g t -> p (v g t)").bitcast(FP8X4),
+                scales=h_planes[:, b].rearrange("p v g t -> p (v g t)"),
+                in_=shifted[:].rearrange("p v g w k -> p (v g w k)"),
+            )
 
         def move_rows(b):
             rows = row_words[:, b].bitcast(I32).rearrange("p g (w h) -> p g w h", h=H)
             nc.vector.tensor_copy(out=rows[:, :, 0 : W + 2 : W + 1, :], in_=rows[:, :, 1 : W + 1 : W - 1, :])
-            same, down, up = (
-                x_planes[v][:, b].bitcast(I32).rearrange("p g (w k) -> p g w k", w=W) for v in (SAME, W_MINUS, W_PLUS)
-            )
-            nc.vector.tensor_copy(out=down[:, :, 1:W, :], in_=same[:, :, 0 : W - 1, :])
-            nc.vector.tensor_copy(out=down[:, :, 0:1, :], in_=same[:, :, 0:1, :])
-            nc.vector.tensor_copy(out=up[:, :, 0 : W - 1, :], in_=same[:, :, 1:W, :])
-            nc.vector.tensor_copy(out=up[:, :, W - 1 : W, :], in_=same[:, :, W - 1 : W, :])
+            same = same_planes[:, b].bitcast(I32).rearrange("p g (w k) -> p g w k", w=W)
+            both = w_shift_planes[:, b].rearrange("p g v t -> p g (v t)").bitcast(I32).rearrange("p g (r k) -> p g r k", r=2 * W)
+            nc.vector.tensor_copy(out=both[:, :, 1:W, :], in_=same[:, :, 0 : W - 1, :])
+            nc.vector.tensor_copy(out=both[:, :, W : 2 * W - 1, :], in_=same[:, :, 1:W, :])
+            nc.vector.tensor_copy(out=both[:, :, 0 : 2 * W : 2 * W - 1, :], in_=same[:, :, 0 : W : W - 1, :])
 
         def product(b, version, words, planes):
             acc = banks.tile([P, BANK], F32)
@@ -191,7 +205,7 @@ def tile_modelnew_pa_kernel(tc, x, w1_words, w1_scales, b1, out_0, out_1, out_2,
                 nc.tensor.matmul_mx(
                     out=acc[:],
                     lhsT=x_words(version, b, g).bitcast(FP8X4),
-                    lhsT_scale=x_planes[version][:, b, g, :],
+                    lhsT_scale=x_scales(version, b, g),
                     rhs=words[g].bitcast(FP4X4),
                     rhs_scale=planes[g],
                     start=(g == 0),
@@ -238,9 +252,9 @@ def tile_modelnew_pa_kernel(tc, x, w1_words, w1_scales, b1, out_0, out_1, out_2,
                     quarter = slice(shift * QUARTER, (shift + 1) * QUARTER)
                     nc.vector.tensor_tensor(out=z[:, quarter], in0=y3[:, quarter], in1=y12[:, shift, :], op=ADD)
                 if shift == QUANTISE_AFTER and b + AHEAD < B:
-                    grouped, h_minus, h_plus = staged[b + AHEAD]
+                    grouped, shifted = staged[b + AHEAD]
                     quantise_same(b + AHEAD, grouped)
-                    quantise_shifted(b + AHEAD, h_minus, h_plus)
+                    quantise_shifted(b + AHEAD, shifted)
                     move_rows(b + AHEAD)
                     if b + AHEAD + 1 < B:
                         staged[b + AHEAD + 1] = stage_batch(b + AHEAD + 1)
@@ -285,12 +299,12 @@ def tile_modelnew_pa_kernel(tc, x, w1_words, w1_scales, b1, out_0, out_1, out_2,
         ctx.enter_context(tc.manual_schedule())
         staged = {}
         spread = {branch: spread_bias(branch) for branch in (2, 0, 1)}
-        staged[0] = stage_batch(0)
-        quantise_same(0, staged[0][0])
+        grouped, shifted = stage_batch(0)
+        quantise_same(0, grouped)
         keep_bias(2, spread[2], nc.vector.tensor_copy)
-        pair_scale_bytes()
         move_rows(0)
-        quantise_shifted(0, staged[0][1], staged[0][2])
+        quantise_shifted(0, shifted)
+        pair_scale_bytes()
         keep_bias(0, spread[0], nc.scalar.copy)
         keep_bias(1, spread[1], nc.scalar.copy)
         staged[1] = stage_batch(1)

@@ -26,6 +26,7 @@ TOKEN_WORDS = PACK // 2
 AHEAD = 1
 LATE = 1
 QUANTISE_AFTER = 2
+WARM_UP = 4
 
 FLOPS = 2 * B * T * C * O
 
@@ -52,7 +53,8 @@ def tile_modelnew_pa_kernel(tc, x, w1_words, w1_scales, b1, out_0, out_1, out_2,
         turns = ctx.enter_context(tc.psum_pool(name="turns", bufs=4))
 
         raw = keep.tile([P, B, G, PACK, T], BF16)
-        w_planes = keep.tile([P, G, O], U8, align_bytes=64)
+        x3_planes = keep.tile([P, G, C], U8, align_bytes=64)
+        x12_planes = keep.tile([P, G, 2 * C], U8, align_bytes=64)
         x3_words = keep.tile([P, G, 2 * C], U8, align_bytes=64)
         pair_words = keep.tile([P, G, 4, 2, 2 * QUARTER], U8, align_bytes=64)
         pair_planes = keep.tile([P, G, 4, 2, QUARTER], U8, align_bytes=64)
@@ -79,12 +81,15 @@ def tile_modelnew_pa_kernel(tc, x, w1_words, w1_scales, b1, out_0, out_1, out_2,
         identity = keep.tile([P, P], F32)
         identity_bf16 = keep.tile([P, P], BF16)
         bias_seed = keep.tile([P, BANK], BF16)
+        zeros = keep.tile([P, BANK], BF16)
         unread = keep.tile([P, BLOCKS, 2 * P], BF16)
         a_by_channel = keep.tile([P, P], F32)
         a_rows = keep.tile([P, P], F32)
 
-        nc.gpsimd.memset(bias_seed[:], 0.0)
-        nc.vector.memset(w_planes[:].bitcast(I32), 0)
+        nc.vector.memset(bias_seed[:].bitcast(F32), 0.0)
+        nc.gpsimd.memset(zeros[:].bitcast(F32), 0.0)
+        nc.vector.memset(x3_planes[:].bitcast(I32), 0)
+        nc.vector.memset(x12_planes[:].bitcast(I32), 0)
         nc.gpsimd.memset(a_by_channel[:], 0.0)
         make_identity(nc, identity_bf16[:])
         make_identity(nc, identity[:])
@@ -105,6 +110,13 @@ def tile_modelnew_pa_kernel(tc, x, w1_words, w1_scales, b1, out_0, out_1, out_2,
                         in_=w1_words[g, :, first : first + 4 * QUARTER].rearrange("p (s k) -> p s k", s=2).bitcast(I32),
                     )
 
+        def load_scales(planes, first):
+            for r in range(4):
+                nc.sync.dma_start(
+                    out=planes[r : P : 32, :, :].bitcast(I32),
+                    in_=w1_scales[:, r : 16 : 4, first : first + planes.shape[2]].rearrange("g q n -> q g n").bitcast(I32),
+                )
+
         load_x(0)
         bias_by_row = b1.rearrange("(i n) -> i n", n=BANK)
         nc.sync.dma_start(out=bias_seed[4:6, :], in_=bias_by_row[4:6, :])
@@ -113,16 +125,18 @@ def tile_modelnew_pa_kernel(tc, x, w1_words, w1_scales, b1, out_0, out_1, out_2,
             out=x3_words[:].bitcast(I32),
             in_=w1_words.rearrange("g p n -> p g n")[:, :, 4 * C : 6 * C].bitcast(I32),
         )
-        for r in range(4):
-            nc.sync.dma_start(
-                out=w_planes[r : P : 32, :, :].bitcast(I32),
-                in_=w1_scales[:, r : 16 : 4, :].rearrange("g q n -> q g n").bitcast(I32),
-            )
+        load_scales(x3_planes, 2 * C)
+        load_scales(x12_planes, 0)
         load_pair_words(0)
         load_x(1)
         load_pair_words(2)
         for b in range(2, B):
             load_x(b)
+
+        def keep_tensor_busy():
+            for i in range(WARM_UP):
+                idle = banks.tile([P, BANK], F32, name="acc")
+                nc.tensor.matmul(out=idle[:], lhsT=zeros[:, 0:P], rhs=zeros[:], start=True, stop=True)
 
         def spread_bias(branch):
             spread = turns.tile([P, C], BF16, tag="turned")
@@ -143,13 +157,13 @@ def tile_modelnew_pa_kernel(tc, x, w1_words, w1_scales, b1, out_0, out_1, out_2,
         def pair_scale_bytes():
             nc.vector.tensor_copy(
                 out=pair_planes[:, :, :, 0, :].bitcast(I32),
-                in_=w_planes[:, :, 0:C].rearrange("p g (s c) -> p g s c", s=4).bitcast(I32),
+                in_=x12_planes[:, :, 0:C].rearrange("p g (s c) -> p g s c", s=4).bitcast(I32),
             )
             for shift in (0, 2):
                 first = C + x2_quarter(shift) * QUARTER
                 nc.vector.tensor_copy(
                     out=pair_planes[:, :, shift : shift + 2, 1, :].bitcast(I32),
-                    in_=w_planes[:, :, first : first + 2 * QUARTER].rearrange("p g (s c) -> p g s c", s=2).bitcast(I32),
+                    in_=x12_planes[:, :, first : first + 2 * QUARTER].rearrange("p g (s c) -> p g s c", s=2).bitcast(I32),
                 )
 
         def interleave(b):
@@ -200,7 +214,7 @@ def tile_modelnew_pa_kernel(tc, x, w1_words, w1_scales, b1, out_0, out_1, out_2,
             nc.vector.tensor_copy(out=both[:, :, 0 : 2 * W : 2 * W - 1, :], in_=same[:, :, 0 : W : W - 1, :])
 
         def product(b, version, words, planes):
-            acc = banks.tile([P, BANK], F32)
+            acc = banks.tile([P, BANK], F32, name="acc")
             for g in range(G):
                 nc.tensor.matmul_mx(
                     out=acc[:],
@@ -213,6 +227,15 @@ def tile_modelnew_pa_kernel(tc, x, w1_words, w1_scales, b1, out_0, out_1, out_2,
                 )
             return acc
 
+        def store_quarters(b, y12, first, last):
+            rows = slice(b * T, (b + 1) * T)
+            for out, branch, quarter in ((out_0, 0, first), (out_1, 4, x2_quarter(first))):
+                n = last - first
+                nc.sync.dma_start(
+                    out=out.rearrange("b w h c -> (b w h) c")[rows, quarter * QUARTER : (quarter + n) * QUARTER],
+                    in_=y12[:, branch + quarter : branch + quarter + n, :].rearrange("p q c -> p (q c)"),
+                )
+
         def project_batch(b):
             rows = slice(b * T, (b + 1) * T)
             y3 = results.tile([P, C], F32)
@@ -221,7 +244,7 @@ def tile_modelnew_pa_kernel(tc, x, w1_words, w1_scales, b1, out_0, out_1, out_2,
                     b,
                     SAME,
                     [x3_words[:, g, 2 * c0 : 2 * (c0 + BANK)] for g in range(G)],
-                    [w_planes[:, g, 2 * C + c0 : 2 * C + c0 + BANK] for g in range(G)],
+                    [x3_planes[:, g, c0 : c0 + BANK] for g in range(G)],
                 )
                 nc.vector.tensor_tensor(
                     out=y3[:, c0 : c0 + BANK],
@@ -250,7 +273,11 @@ def tile_modelnew_pa_kernel(tc, x, w1_words, w1_scales, b1, out_0, out_1, out_2,
                 )
                 if b == B - 1:
                     quarter = slice(shift * QUARTER, (shift + 1) * QUARTER)
-                    nc.vector.tensor_tensor(out=z[:, quarter], in0=y3[:, quarter], in1=y12[:, shift, :], op=ADD)
+                    engine = nc.vector if shift == SHIFTS[-1] else nc.gpsimd
+                    engine.tensor_tensor(out=z[:, quarter], in0=y3[:, quarter], in1=y12[:, shift, :], op=ADD)
+                    if shift >= 1:
+                        first = 0 if shift == 1 else shift
+                        store_quarters(b, y12, first, shift + 1)
                 if shift == QUANTISE_AFTER and b + AHEAD < B:
                     grouped, shifted = staged[b + AHEAD]
                     quantise_same(b + AHEAD, grouped)
@@ -260,44 +287,64 @@ def tile_modelnew_pa_kernel(tc, x, w1_words, w1_scales, b1, out_0, out_1, out_2,
                         staged[b + AHEAD + 1] = stage_batch(b + AHEAD + 1)
             y1 = y12[:, 0:4, :].rearrange("p q c -> p (q c)")
             y2 = y12[:, 4:8, :].rearrange("p q c -> p (q c)")
-            nc.sync.dma_start(out=out_0.rearrange("b w h c -> (b w h) c")[rows, :], in_=y1)
-            nc.sync.dma_start(out=out_1.rearrange("b w h c -> (b w h) c")[rows, :], in_=y2)
             if b < B - 1:
+                nc.sync.dma_start(out=out_0.rearrange("b w h c -> (b w h) c")[rows, :], in_=y1)
+                nc.sync.dma_start(out=out_1.rearrange("b w h c -> (b w h) c")[rows, :], in_=y2)
                 nc.gpsimd.tensor_tensor(out=z[:], in0=y3[:], in1=y1, op=ADD)
             return y2, z[:]
 
+        def sum_by_scalar(b, i, turned):
+            nc.scalar.activation(
+                out=unread[:, i, 0 : turned.shape[1]],
+                in_=turned,
+                func=COPY,
+                accum_out=a_by_channel[:, b * BLOCKS + i : b * BLOCKS + i + 1],
+            )
+
         def sum_tokens(b, parts):
+            turned = [turns.tile([P, 2, 2, P], F32, name="turned") for quarter in range(4)]
+            for n in range(2):
+                for i in range(BLOCKS):
+                    nc.tensor.transpose(turned[i // 2][:, i % 2, n, :], parts[n][:, i * P : (i + 1) * P], identity[:])
+            for i in range(BLOCKS):
+                sum_by_scalar(b, i, turned[i // 2][:, i % 2].rearrange("p n t -> p (n t)"))
+
+        def turn_and_add(out, parts, i):
+            for n in range(2):
+                nc.tensor.matmul(
+                    out=out,
+                    lhsT=parts[n][:, i * P : (i + 1) * P],
+                    rhs=identity[:],
+                    is_transpose=True,
+                    start=(n == 0),
+                    stop=(n == 1),
+                )
+
+        def sum_tokens_at_end(b, parts):
             if b < B - 1:
-                turned = [turns.tile([P, 2, 2, P], F32, name="turned") for quarter in range(4)]
-                order = [(n, i) for n in range(2) for i in range(BLOCKS)]
-                quarters = range(4)
-            else:
-                turned = [banks.tile([P, 2, 2, P], F32, name="acc") for quarter in range(4)]
-                order = [(n, 2 * quarter + i) for quarter in QUARTER_ORDER for n in range(2) for i in range(2)]
-                quarters = QUARTER_ORDER
-            for n, i in order:
-                nc.tensor.transpose(turned[i // 2][:, i % 2, n, :], parts[n][:, i * P : (i + 1) * P], identity[:])
-            vector_quarters = (2, 3) if b >= B - 1 - LATE else ()
-            for quarter in quarters:
-                first = b * BLOCKS + 2 * quarter
-                if quarter in vector_quarters:
+                turned = [turns.tile([P, 4, P], F32, name="turned") for half in range(2)]
+                for i in range(BLOCKS):
+                    turn_and_add(turned[i // 4][:, i % 4, :], parts, i)
+                for i in range(BLOCKS):
+                    sum_by_scalar(b, i, turned[i // 4][:, i % 4, :])
+                return
+            turned = [banks.tile([P, 2, P], F32, name="acc") for quarter in range(4)]
+            for quarter in QUARTER_ORDER:
+                for i in range(2):
+                    turn_and_add(turned[quarter][:, i, :], parts, 2 * quarter + i)
+            for quarter in QUARTER_ORDER:
+                if quarter == QUARTER_ORDER[-1]:
+                    first = b * BLOCKS + 2 * quarter
                     nc.vector.tensor_reduce(
-                        out=a_by_channel[:, first : first + 2],
-                        in_=turned[quarter][:].rearrange("p i n t -> p i (n t)"),
-                        op=ADD,
-                        axis=mybir.AxisListType.X,
+                        out=a_by_channel[:, first : first + 2], in_=turned[quarter][:], op=ADD, axis=mybir.AxisListType.X
                     )
                     continue
                 for i in range(2):
-                    nc.scalar.activation(
-                        out=unread[:, 2 * quarter + i, :],
-                        in_=turned[quarter][:, i].rearrange("p n t -> p (n t)"),
-                        func=COPY,
-                        accum_out=a_by_channel[:, first + i : first + i + 1],
-                    )
+                    sum_by_scalar(b, 2 * quarter + i, turned[quarter][:, i, :])
 
         ctx.enter_context(tc.manual_schedule())
         staged = {}
+        keep_tensor_busy()
         spread = {branch: spread_bias(branch) for branch in (2, 0, 1)}
         grouped, shifted = stage_batch(0)
         quantise_same(0, grouped)
@@ -312,9 +359,9 @@ def tile_modelnew_pa_kernel(tc, x, w1_words, w1_scales, b1, out_0, out_1, out_2,
         for b in range(B):
             parts_of_batch.append(project_batch(b))
             if b >= LATE:
-                sum_tokens(b - LATE, parts_of_batch[b - LATE])
+                (sum_tokens if b < B - 1 else sum_tokens_at_end)(b - LATE, parts_of_batch[b - LATE])
         for b in range(B - LATE, B):
-            sum_tokens(b, parts_of_batch[b])
+            sum_tokens_at_end(b, parts_of_batch[b])
 
         a_turned = turns.tile([P, P], F32, tag="turned")
         nc.tensor.transpose(a_turned[:], a_by_channel[:], identity[:])

@@ -53,8 +53,7 @@ def tile_modelnew_pa_kernel(tc, x, w1_words, w1_scales, b1, out_0, out_1, out_2,
         turns = ctx.enter_context(tc.psum_pool(name="turns", bufs=4))
 
         raw = keep.tile([P, B, G, PACK, T], BF16)
-        x3_planes = keep.tile([P, G, C], U8, align_bytes=64)
-        x12_planes = keep.tile([P, G, 2 * C], U8, align_bytes=64)
+        w_planes = keep.tile([P, G, O], U8, align_bytes=64)
         x3_words = keep.tile([P, G, 2 * C], U8, align_bytes=64)
         pair_words = keep.tile([P, G, 4, 2, 2 * QUARTER], U8, align_bytes=64)
         pair_planes = keep.tile([P, G, 4, 2, QUARTER], U8, align_bytes=64)
@@ -88,36 +87,26 @@ def tile_modelnew_pa_kernel(tc, x, w1_words, w1_scales, b1, out_0, out_1, out_2,
 
         nc.vector.memset(bias_seed[:].bitcast(F32), 0.0)
         nc.gpsimd.memset(zeros[:].bitcast(F32), 0.0)
-        nc.vector.memset(x3_planes[:].bitcast(I32), 0)
-        nc.vector.memset(x12_planes[:].bitcast(I32), 0)
-        nc.gpsimd.memset(a_by_channel[:], 0.0)
+        nc.vector.memset(w_planes[:].bitcast(I32), 0)
         make_identity(nc, identity_bf16[:])
-        make_identity(nc, identity[:])
 
-        def load_x(b):
-            nc.sync.dma_start(
+        def load_x(b, queue):
+            queue.dma_start(
                 out=raw[:, b],
                 in_=x[b].rearrange("(g p j) w h -> p g j (w h)", g=G, p=P, j=PACK),
             )
 
-        def load_pair_words(first_shift):
-            shifts = slice(first_shift, first_shift + 2)
+        def load_pair_words(branch, shifts, first_quarter):
+            first = 2 * first_quarter * QUARTER
+            n = shifts.stop - shifts.start
             for g in range(G):
-                for branch, first_quarter in ((0, first_shift), (1, 4 + x2_quarter(first_shift))):
-                    first = 2 * first_quarter * QUARTER
-                    nc.sync.dma_start(
-                        out=pair_words[:, g, shifts, branch, :].bitcast(I32),
-                        in_=w1_words[g, :, first : first + 4 * QUARTER].rearrange("p (s k) -> p s k", s=2).bitcast(I32),
-                    )
-
-        def load_scales(planes, first):
-            for r in range(4):
                 nc.sync.dma_start(
-                    out=planes[r : P : 32, :, :].bitcast(I32),
-                    in_=w1_scales[:, r : 16 : 4, first : first + planes.shape[2]].rearrange("g q n -> q g n").bitcast(I32),
+                    out=pair_words[:, g, shifts, branch, :].bitcast(I32),
+                    in_=w1_words[g, :, first : first + 2 * n * QUARTER].rearrange("p (s k) -> p s k", s=n).bitcast(I32),
                 )
 
-        load_x(0)
+        load_x(1, nc.gpsimd)
+        load_x(0, nc.sync)
         bias_by_row = b1.rearrange("(i n) -> i n", n=BANK)
         nc.sync.dma_start(out=bias_seed[4:6, :], in_=bias_by_row[4:6, :])
         nc.sync.dma_start(out=bias_seed[0:4, :], in_=bias_by_row[0:4, :])
@@ -125,13 +114,19 @@ def tile_modelnew_pa_kernel(tc, x, w1_words, w1_scales, b1, out_0, out_1, out_2,
             out=x3_words[:].bitcast(I32),
             in_=w1_words.rearrange("g p n -> p g n")[:, :, 4 * C : 6 * C].bitcast(I32),
         )
-        load_scales(x3_planes, 2 * C)
-        load_scales(x12_planes, 0)
-        load_pair_words(0)
-        load_x(1)
-        load_pair_words(2)
+        for r in range(4):
+            nc.sync.dma_start(
+                out=w_planes[r : P : 32, :, :].bitcast(I32),
+                in_=w1_scales[:, r : 16 : 4, :].rearrange("g q n -> q g n").bitcast(I32),
+            )
+        load_pair_words(0, slice(0, 4), 0)
+        for shift in (0, 2):
+            load_pair_words(1, slice(shift, shift + 2), 4 + x2_quarter(shift))
         for b in range(2, B):
-            load_x(b)
+            load_x(b, nc.sync)
+
+        nc.gpsimd.memset(a_by_channel[:], 0.0)
+        make_identity(nc, identity[:])
 
         def keep_tensor_busy():
             for i in range(WARM_UP):
@@ -157,13 +152,13 @@ def tile_modelnew_pa_kernel(tc, x, w1_words, w1_scales, b1, out_0, out_1, out_2,
         def pair_scale_bytes():
             nc.vector.tensor_copy(
                 out=pair_planes[:, :, :, 0, :].bitcast(I32),
-                in_=x12_planes[:, :, 0:C].rearrange("p g (s c) -> p g s c", s=4).bitcast(I32),
+                in_=w_planes[:, :, 0:C].rearrange("p g (s c) -> p g s c", s=4).bitcast(I32),
             )
             for shift in (0, 2):
                 first = C + x2_quarter(shift) * QUARTER
                 nc.vector.tensor_copy(
                     out=pair_planes[:, :, shift : shift + 2, 1, :].bitcast(I32),
-                    in_=x12_planes[:, :, first : first + 2 * QUARTER].rearrange("p g (s c) -> p g s c", s=2).bitcast(I32),
+                    in_=w_planes[:, :, first : first + 2 * QUARTER].rearrange("p g (s c) -> p g s c", s=2).bitcast(I32),
                 )
 
         def interleave(b):
@@ -244,7 +239,7 @@ def tile_modelnew_pa_kernel(tc, x, w1_words, w1_scales, b1, out_0, out_1, out_2,
                     b,
                     SAME,
                     [x3_words[:, g, 2 * c0 : 2 * (c0 + BANK)] for g in range(G)],
-                    [x3_planes[:, g, c0 : c0 + BANK] for g in range(G)],
+                    [w_planes[:, g, 2 * C + c0 : 2 * C + c0 + BANK] for g in range(G)],
                 )
                 nc.vector.tensor_tensor(
                     out=y3[:, c0 : c0 + BANK],

@@ -23,6 +23,7 @@ QUARTER = C // 4
 BANK = 512
 BLOCKS = C // P
 TOKEN_WORDS = PACK // 2
+WORDS = G * T * TOKEN_WORDS
 AHEAD = 1
 LATE = 1
 QUANTISE_AFTER = 2
@@ -57,7 +58,7 @@ def tile_modelnew_pa_kernel(tc, x, w1_words, w1_scales, b1, out_0, out_1, out_2,
         x3_words = keep.tile([P, G, 2 * C], U8, align_bytes=64)
         pair_words = keep.tile([P, G, 4, 2, 2 * QUARTER], U8, align_bytes=64)
         pair_planes = keep.tile([P, G, 4, 2, QUARTER], U8, align_bytes=64)
-        bias_rows = keep.tile([P, O // QUARTER, QUARTER], BF16)
+        bias_rows = keep.tile([P, O // QUARTER, QUARTER], F32)
         row_words = keep.tile([P, B, G, T + 2 * H], U32, align_bytes=64)
         h_words = keep.tile([P, B, 2, G, T], U32, align_bytes=64)
         same_planes = keep.tile([P, B, G, T], U8, align_bytes=64)
@@ -163,26 +164,31 @@ def tile_modelnew_pa_kernel(tc, x, w1_words, w1_scales, b1, out_0, out_1, out_2,
 
         def interleave(b):
             grouped = stage.tile([P, G, T, PACK], BF16, align_bytes=64)
-            copy = nc.vector.tensor_copy if b == 0 else nc.scalar.copy
-            copy(out=grouped[:], in_=raw[:, b].rearrange("p g j t -> p g t j"))
+            if b == 0:
+                nc.vector.tensor_copy(out=grouped[:], in_=raw[:, b].rearrange("p g j t -> p g t j"))
+            else:
+                nc.scalar.copy(
+                    out=grouped[:].rearrange("p g (c i) j -> p g c j i", i=4),
+                    in_=raw[:, b].rearrange("p g j (c i) -> p g c j i", i=4),
+                )
             return grouped
 
         def shift_in_h(grouped):
-            row = TOKEN_WORDS * H
-            last = row - TOKEN_WORDS
-            grid = grouped[:].rearrange("p g t j -> p g (t j)").bitcast(F32).rearrange("p g (w k) -> p g w k", k=row)
-            shifted = stage.tile([P, 2, G, W, H * PACK], BF16, align_bytes=64)
-            h_minus = shifted[:, 0].bitcast(F32)
-            h_plus = shifted[:, 1].bitcast(F32)
-            nc.scalar.copy(out=h_minus[:, :, :, TOKEN_WORDS:row], in_=grid[:, :, :, 0:last])
-            nc.scalar.copy(out=h_minus[:, :, :, 0:TOKEN_WORDS], in_=grid[:, :, :, 0:TOKEN_WORDS])
-            nc.scalar.copy(out=h_plus[:, :, :, 0:last], in_=grid[:, :, :, TOKEN_WORDS:row])
-            nc.scalar.copy(out=h_plus[:, :, :, last:row], in_=grid[:, :, :, last:row])
+            flat = grouped[:].rearrange("p g t j -> p (g t j)").bitcast(F32)
+            shifted = stage.tile([P, 2, G, T * PACK], BF16, align_bytes=64)
+            h_minus, h_plus = words_of(shifted)
+            nc.scalar.copy(out=h_minus[:, TOKEN_WORDS:WORDS], in_=flat[:, 0 : WORDS - TOKEN_WORDS])
+            nc.scalar.copy(out=h_plus[:, 0 : WORDS - TOKEN_WORDS], in_=flat[:, TOKEN_WORDS:WORDS])
             return shifted
 
-        def stage_batch(b):
-            grouped = interleave(b)
-            return grouped, shift_in_h(grouped)
+        def words_of(shifted):
+            return [shifted[:, i].rearrange("p g k -> p (g k)").bitcast(F32) for i in range(2)]
+
+        def set_edges(grouped, shifted):
+            flat = grouped[:].rearrange("p g t j -> p (g t j)").bitcast(F32)
+            for moved, h in zip(words_of(shifted), (0, H - 1)):
+                edge_of = lambda words: words.rearrange("p (r k) -> p r k", k=TOKEN_WORDS * H)[:, :, TOKEN_WORDS * h : TOKEN_WORDS * (h + 1)]
+                nc.scalar.copy(out=edge_of(moved), in_=edge_of(flat))
 
         def quantise_same(b, grouped):
             for g in range(G):
@@ -196,7 +202,7 @@ def tile_modelnew_pa_kernel(tc, x, w1_words, w1_scales, b1, out_0, out_1, out_2,
             nc.vector.quantize_mx(
                 out=h_words[:, b].rearrange("p v g t -> p (v g t)").bitcast(FP8X4),
                 scales=h_planes[:, b].rearrange("p v g t -> p (v g t)"),
-                in_=shifted[:].rearrange("p v g w k -> p (v g w k)"),
+                in_=shifted[:].rearrange("p v g k -> p (v g k)"),
             )
 
         def move_rows(b):
@@ -274,12 +280,15 @@ def tile_modelnew_pa_kernel(tc, x, w1_words, w1_scales, b1, out_0, out_1, out_2,
                         first = 0 if shift == 1 else shift
                         store_quarters(b, y12, first, shift + 1)
                 if shift == QUANTISE_AFTER and b + AHEAD < B:
-                    grouped, shifted = staged[b + AHEAD]
-                    quantise_same(b + AHEAD, grouped)
-                    quantise_shifted(b + AHEAD, shifted)
+                    quantise_same(b + AHEAD, grouped[b + AHEAD])
+                    quantise_shifted(b + AHEAD, shifted[b + AHEAD])
                     move_rows(b + AHEAD)
-                    if b + AHEAD + 1 < B:
-                        staged[b + AHEAD + 1] = stage_batch(b + AHEAD + 1)
+                    later = b + AHEAD + 1
+                    if later < B:
+                        shifted[later] = shift_in_h(grouped[later])
+                        if later + 1 < B:
+                            grouped[later + 1] = interleave(later + 1)
+                        set_edges(grouped[later], shifted[later])
             y1 = y12[:, 0:4, :].rearrange("p q c -> p (q c)")
             y2 = y12[:, 4:8, :].rearrange("p q c -> p (q c)")
             if b < B - 1:
@@ -338,18 +347,23 @@ def tile_modelnew_pa_kernel(tc, x, w1_words, w1_scales, b1, out_0, out_1, out_2,
                     sum_by_scalar(b, 2 * quarter + i, turned[quarter][:, i, :])
 
         ctx.enter_context(tc.manual_schedule())
-        staged = {}
+        grouped, shifted = {}, {}
         keep_tensor_busy()
         spread = {branch: spread_bias(branch) for branch in (2, 0, 1)}
-        grouped, shifted = stage_batch(0)
-        quantise_same(0, grouped)
+        grouped[0] = interleave(0)
+        quantise_same(0, grouped[0])
+        shifted[0] = shift_in_h(grouped[0])
+        set_edges(grouped[0], shifted[0])
         keep_bias(2, spread[2], nc.vector.tensor_copy)
         move_rows(0)
-        quantise_shifted(0, shifted)
+        quantise_shifted(0, shifted[0])
         pair_scale_bytes()
         keep_bias(0, spread[0], nc.scalar.copy)
         keep_bias(1, spread[1], nc.scalar.copy)
-        staged[1] = stage_batch(1)
+        grouped[1] = interleave(1)
+        shifted[1] = shift_in_h(grouped[1])
+        set_edges(grouped[1], shifted[1])
+        grouped[2] = interleave(2)
         parts_of_batch = []
         for b in range(B):
             parts_of_batch.append(project_batch(b))

@@ -58,11 +58,11 @@ def tile_modelnew_pa_kernel(tc, x, w1_words, w1_scales, b1, out_0, out_1, out_2,
         x3_words = keep.tile([P, G, 2 * C], U8, align_bytes=64)
         pair_words = keep.tile([P, G, 4, 2, 2 * QUARTER], U8, align_bytes=64)
         pair_planes = keep.tile([P, G, 4, 2, QUARTER], U8, align_bytes=64)
-        bias_rows = keep.tile([P, O // QUARTER, QUARTER], F32)
+        bias_rows = keep.tile([P, O // QUARTER, QUARTER], BF16)
         row_words = keep.tile([P, B, G, T + 2 * H], U32, align_bytes=64)
         h_words = keep.tile([P, B, 2, G, T], U32, align_bytes=64)
         same_planes = keep.tile([P, B, G, T], U8, align_bytes=64)
-        w_shift_planes = keep.tile([P, B, G, 2, T], U8, align_bytes=64)
+        w_shift_planes = keep.tile([P, B, G, 2 * T], U8, align_bytes=64)
         h_planes = keep.tile([P, B, 2, G, T], U8, align_bytes=64)
         window_start = {W_MINUS: 0, SAME: H, W_PLUS: 2 * H}
 
@@ -75,7 +75,7 @@ def tile_modelnew_pa_kernel(tc, x, w1_words, w1_scales, b1, out_0, out_1, out_2,
             if version == SAME:
                 return same_planes[:, b, g, :]
             if version in window_start:
-                return w_shift_planes[:, b, g, version - W_MINUS, :]
+                return w_shift_planes[:, b, g, (version - W_MINUS) * T : (version - W_MINUS + 1) * T]
             return h_planes[:, b, version - H_MINUS, g, :]
 
         identity = keep.tile([P, P], F32)
@@ -165,7 +165,8 @@ def tile_modelnew_pa_kernel(tc, x, w1_words, w1_scales, b1, out_0, out_1, out_2,
         def interleave(b):
             grouped = stage.tile([P, G, T, PACK], BF16, align_bytes=64)
             if b == 0:
-                nc.vector.tensor_copy(out=grouped[:], in_=raw[:, b].rearrange("p g j t -> p g t j"))
+                for g, copy in ((0, nc.vector.tensor_copy), (1, nc.scalar.copy)):
+                    copy(out=grouped[:, g], in_=raw[:, b, g].rearrange("p j t -> p t j"))
             else:
                 nc.scalar.copy(
                     out=grouped[:].rearrange("p g (c i) j -> p g c j i", i=4),
@@ -205,11 +206,14 @@ def tile_modelnew_pa_kernel(tc, x, w1_words, w1_scales, b1, out_0, out_1, out_2,
                 in_=shifted[:].rearrange("p v g k -> p (v g k)"),
             )
 
-        def move_rows(b):
-            rows = row_words[:, b].bitcast(I32).rearrange("p g (w h) -> p g w h", h=H)
+        def move_rows(batches):
+            def as_rows(tile, rows):
+                return tile[:, batches].rearrange("p b g k -> p (b g k)").bitcast(I32).rearrange("p (r w k) -> p r w k", r=G * len(range(B)[batches]), w=rows)
+
+            rows = as_rows(row_words, W + 2)
             nc.vector.tensor_copy(out=rows[:, :, 0 : W + 2 : W + 1, :], in_=rows[:, :, 1 : W + 1 : W - 1, :])
-            same = same_planes[:, b].bitcast(I32).rearrange("p g (w k) -> p g w k", w=W)
-            both = w_shift_planes[:, b].rearrange("p g v t -> p g (v t)").bitcast(I32).rearrange("p g (r k) -> p g r k", r=2 * W)
+            same = as_rows(same_planes, W)
+            both = as_rows(w_shift_planes, 2 * W)
             nc.vector.tensor_copy(out=both[:, :, 1:W, :], in_=same[:, :, 0 : W - 1, :])
             nc.vector.tensor_copy(out=both[:, :, W : 2 * W - 1, :], in_=same[:, :, 1:W, :])
             nc.vector.tensor_copy(out=both[:, :, 0 : 2 * W : 2 * W - 1, :], in_=same[:, :, 0 : W : W - 1, :])
@@ -280,9 +284,13 @@ def tile_modelnew_pa_kernel(tc, x, w1_words, w1_scales, b1, out_0, out_1, out_2,
                         first = 0 if shift == 1 else shift
                         store_quarters(b, y12, first, shift + 1)
                 if shift == QUANTISE_AFTER and b + AHEAD < B:
-                    quantise_same(b + AHEAD, grouped[b + AHEAD])
+                    pair = slice(1, 2) if b == 0 else slice(b + 1, b + 3) if b % 2 else None
+                    if pair:
+                        for k in range(B)[pair]:
+                            quantise_same(k, grouped[k])
                     quantise_shifted(b + AHEAD, shifted[b + AHEAD])
-                    move_rows(b + AHEAD)
+                    if pair:
+                        move_rows(pair)
                     later = b + AHEAD + 1
                     if later < B:
                         shifted[later] = shift_in_h(grouped[later])
@@ -354,8 +362,8 @@ def tile_modelnew_pa_kernel(tc, x, w1_words, w1_scales, b1, out_0, out_1, out_2,
         quantise_same(0, grouped[0])
         shifted[0] = shift_in_h(grouped[0])
         set_edges(grouped[0], shifted[0])
-        keep_bias(2, spread[2], nc.vector.tensor_copy)
-        move_rows(0)
+        keep_bias(2, spread[2], nc.scalar.copy)
+        move_rows(slice(0, 1))
         quantise_shifted(0, shifted[0])
         pair_scale_bytes()
         keep_bias(0, spread[0], nc.scalar.copy)

@@ -174,22 +174,22 @@ def tile_modelnew_pa_kernel(tc, x, w1_words, w1_scales, b1, out_0, out_1, out_2,
                 )
             return grouped
 
-        def shift_in_h(grouped):
+        def shift_in_h(grouped, copy):
             flat = grouped[:].rearrange("p g t j -> p (g t j)").bitcast(F32)
             shifted = stage.tile([P, 2, G, T * PACK], BF16, align_bytes=64)
             h_minus, h_plus = words_of(shifted)
-            nc.scalar.copy(out=h_minus[:, TOKEN_WORDS:WORDS], in_=flat[:, 0 : WORDS - TOKEN_WORDS])
-            nc.scalar.copy(out=h_plus[:, 0 : WORDS - TOKEN_WORDS], in_=flat[:, TOKEN_WORDS:WORDS])
+            copy(out=h_minus[:, TOKEN_WORDS:WORDS], in_=flat[:, 0 : WORDS - TOKEN_WORDS])
+            copy(out=h_plus[:, 0 : WORDS - TOKEN_WORDS], in_=flat[:, TOKEN_WORDS:WORDS])
             return shifted
 
         def words_of(shifted):
             return [shifted[:, i].rearrange("p g k -> p (g k)").bitcast(F32) for i in range(2)]
 
-        def set_edges(grouped, shifted):
+        def set_edges(grouped, shifted, copy):
             flat = grouped[:].rearrange("p g t j -> p (g t j)").bitcast(F32)
             for moved, h in zip(words_of(shifted), (0, H - 1)):
                 edge_of = lambda words: words.rearrange("p (r k) -> p r k", k=TOKEN_WORDS * H)[:, :, TOKEN_WORDS * h : TOKEN_WORDS * (h + 1)]
-                nc.scalar.copy(out=edge_of(moved), in_=edge_of(flat))
+                copy(out=edge_of(moved), in_=edge_of(flat))
 
         def quantise_same(b, grouped):
             for g in range(G):
@@ -278,7 +278,7 @@ def tile_modelnew_pa_kernel(tc, x, w1_words, w1_scales, b1, out_0, out_1, out_2,
                 )
                 if b == B - 1:
                     quarter = slice(shift * QUARTER, (shift + 1) * QUARTER)
-                    engine = nc.vector if shift == SHIFTS[-1] else nc.gpsimd
+                    engine = nc.gpsimd if shift < 2 else nc.vector
                     engine.tensor_tensor(out=z[:, quarter], in0=y3[:, quarter], in1=y12[:, shift, :], op=ADD)
                     if shift >= 1:
                         first = 0 if shift == 1 else shift
@@ -293,10 +293,10 @@ def tile_modelnew_pa_kernel(tc, x, w1_words, w1_scales, b1, out_0, out_1, out_2,
                         move_rows(pair)
                     later = b + AHEAD + 1
                     if later < B:
-                        shifted[later] = shift_in_h(grouped[later])
+                        shifted[later] = shift_in_h(grouped[later], nc.scalar.copy)
                         if later + 1 < B:
                             grouped[later + 1] = interleave(later + 1)
-                        set_edges(grouped[later], shifted[later])
+                        set_edges(grouped[later], shifted[later], nc.scalar.copy)
             y1 = y12[:, 0:4, :].rearrange("p q c -> p (q c)")
             y2 = y12[:, 4:8, :].rearrange("p q c -> p (q c)")
             if b < B - 1:
@@ -360,17 +360,17 @@ def tile_modelnew_pa_kernel(tc, x, w1_words, w1_scales, b1, out_0, out_1, out_2,
         spread = {branch: spread_bias(branch) for branch in (2, 0, 1)}
         grouped[0] = interleave(0)
         quantise_same(0, grouped[0])
-        shifted[0] = shift_in_h(grouped[0])
-        set_edges(grouped[0], shifted[0])
-        keep_bias(2, spread[2], nc.scalar.copy)
+        shifted[0] = shift_in_h(grouped[0], nc.vector.tensor_copy)
         move_rows(slice(0, 1))
+        set_edges(grouped[0], shifted[0], nc.vector.tensor_copy)
+        keep_bias(2, spread[2], nc.scalar.copy)
         quantise_shifted(0, shifted[0])
         pair_scale_bytes()
         keep_bias(0, spread[0], nc.scalar.copy)
         keep_bias(1, spread[1], nc.scalar.copy)
         grouped[1] = interleave(1)
-        shifted[1] = shift_in_h(grouped[1])
-        set_edges(grouped[1], shifted[1])
+        shifted[1] = shift_in_h(grouped[1], nc.scalar.copy)
+        set_edges(grouped[1], shifted[1], nc.scalar.copy)
         grouped[2] = interleave(2)
         parts_of_batch = []
         for b in range(B):

from contextlib import ExitStack

import concourse.mybir as mybir
from concourse.masks import make_identity

F32 = mybir.dt.float32
BF16 = mybir.dt.bfloat16
I32 = mybir.dt.int32
U32 = mybir.dt.uint32
U8 = mybir.dt.uint8
FP8X4 = mybir.dt.float8_e4m3fn_x4
FP4X4 = mybir.dt.float4_e2m1fn_x4
ADD = mybir.AluOpType.add
COPY = mybir.ActivationFunctionType.Copy

P = 128
PACK = 4
B, C, W, H = 8, 1024, 8, 16
T = W * H
G = C // (P * PACK)
O = 3 * C
QUARTER = C // 4
BANK = 512
BLOCKS = C // P
TOKEN_WORDS = PACK // 2
WORDS = G * T * TOKEN_WORDS
AHEAD = 1
LATE = 1
QUANTISE_AFTER = 2
WARM_UP = 4

FLOPS = 2 * B * T * C * O

W_MINUS, W_PLUS, H_MINUS, H_PLUS, SAME = range(5)
SHIFTS = (W_MINUS, W_PLUS, H_MINUS, H_PLUS)


QUARTER_ORDER = (0, 2, 1, 3)


def x2_quarter(shift):
    return (shift + 2) % 4


def tile_modelnew_pa_kernel(tc, x, w1_words, w1_scales, b1, out_0, out_1, out_2, out_3):
    nc = tc.nc

    with ExitStack() as ctx:
        keep = ctx.enter_context(tc.tile_pool(name="keep", bufs=1))
        stage = ctx.enter_context(tc.tile_pool(name="stage", bufs=3))
        results = ctx.enter_context(tc.tile_pool(name="results", bufs=3))
        sums = ctx.enter_context(tc.tile_pool(name="sums", bufs=LATE + 2))
        banks = ctx.enter_context(tc.psum_pool(name="banks", bufs=4))
        turns = ctx.enter_context(tc.psum_pool(name="turns", bufs=4))

        raw = keep.tile([P, B, G, PACK, T], BF16)
        w_planes = keep.tile([P, G, O], U8, align_bytes=64)
        x3_words = keep.tile([P, G, 2 * C], U8, align_bytes=64)
        pair_words = keep.tile([P, G, 4, 2, 2 * QUARTER], U8, align_bytes=64)
        pair_planes = keep.tile([P, G, 4, 2, QUARTER], U8, align_bytes=64)
        bias_rows = keep.tile([P, O // QUARTER, QUARTER], BF16)
        row_words = keep.tile([P, B, G, T + 2 * H], U32, align_bytes=64)
        h_words = keep.tile([P, B, 2, G, T], U32, align_bytes=64)
        same_planes = keep.tile([P, B, G, T], U8, align_bytes=64)
        w_shift_planes = keep.tile([P, B, G, 2 * T], U8, align_bytes=64)
        h_planes = keep.tile([P, B, 2, G, T], U8, align_bytes=64)
        window_start = {W_MINUS: 0, SAME: H, W_PLUS: 2 * H}

        def x_words(version, b, g):
            if version in window_start:
                return row_words[:, b, g, window_start[version] : window_start[version] + T]
            return h_words[:, b, version - H_MINUS, g, :]

        def x_scales(version, b, g):
            if version == SAME:
                return same_planes[:, b, g, :]
            if version in window_start:
                return w_shift_planes[:, b, g, (version - W_MINUS) * T : (version - W_MINUS + 1) * T]
            return h_planes[:, b, version - H_MINUS, g, :]

        identity = keep.tile([P, P], F32)
        identity_bf16 = keep.tile([P, P], BF16)
        bias_seed = keep.tile([P, BANK], BF16)
        zeros = keep.tile([P, BANK], BF16)
        unread = keep.tile([P, BLOCKS, 2 * P], BF16)
        a_by_channel = keep.tile([P, P], F32)
        a_rows = keep.tile([P, P], F32)

        nc.vector.memset(bias_seed[:].bitcast(F32), 0.0)
        nc.gpsimd.memset(zeros[:].bitcast(F32), 0.0)
        nc.vector.memset(w_planes[:].bitcast(I32), 0)
        make_identity(nc, identity_bf16[:])

        def load_x(b, queue):
            queue.dma_start(
                out=raw[:, b],
                in_=x[b].rearrange("(g p j) w h -> p g j (w h)", g=G, p=P, j=PACK),
            )

        def load_pair_words(branch, shifts, first_quarter):
            first = 2 * first_quarter * QUARTER
            n = shifts.stop - shifts.start
            for g in range(G):
                nc.sync.dma_start(
                    out=pair_words[:, g, shifts, branch, :].bitcast(I32),
                    in_=w1_words[g, :, first : first + 2 * n * QUARTER].rearrange("p (s k) -> p s k", s=n).bitcast(I32),
                )

        load_x(1, nc.gpsimd)
        load_x(0, nc.sync)
        bias_by_row = b1.rearrange("(i n) -> i n", n=BANK)
        nc.sync.dma_start(out=bias_seed[4:6, :], in_=bias_by_row[4:6, :])
        nc.sync.dma_start(out=bias_seed[0:4, :], in_=bias_by_row[0:4, :])
        nc.sync.dma_start(
            out=x3_words[:].bitcast(I32),
            in_=w1_words.rearrange("g p n -> p g n")[:, :, 4 * C : 6 * C].bitcast(I32),
        )
        for r in range(4):
            nc.sync.dma_start(
                out=w_planes[r : P : 32, :, :].bitcast(I32),
                in_=w1_scales[:, r : 16 : 4, :].rearrange("g q n -> q g n").bitcast(I32),
            )
        load_pair_words(0, slice(0, 4), 0)
        for shift in (0, 2):
            load_pair_words(1, slice(shift, shift + 2), 4 + x2_quarter(shift))
        for b in range(2, B):
            load_x(b, nc.sync)

        nc.gpsimd.memset(a_by_channel[:], 0.0)
        make_identity(nc, identity[:])

        def keep_tensor_busy():
            for i in range(WARM_UP):
                idle = banks.tile([P, BANK], F32, name="acc")
                nc.tensor.matmul(out=idle[:], lhsT=zeros[:, 0:P], rhs=zeros[:], start=True, stop=True)

        def spread_bias(branch):
            spread = turns.tile([P, C], BF16, tag="turned")
            for half in range(C // BANK):
                i = branch * (C // BANK) + half
                nc.tensor.matmul(
                    out=spread[:, half * BANK : (half + 1) * BANK],
                    lhsT=identity_bf16[:, i : i + 1].to_broadcast([P, P]),
                    rhs=bias_seed[:],
                    start=True,
                    stop=True,
                )
            return spread

        def keep_bias(branch, spread, copy):
            copy(out=bias_rows[:, 4 * branch : 4 * branch + 4, :].rearrange("p q c -> p (q c)"), in_=spread[:])

        def pair_scale_bytes():
            nc.vector.tensor_copy(
                out=pair_planes[:, :, :, 0, :].bitcast(I32),
                in_=w_planes[:, :, 0:C].rearrange("p g (s c) -> p g s c", s=4).bitcast(I32),
            )
            for shift in (0, 2):
                first = C + x2_quarter(shift) * QUARTER
                nc.vector.tensor_copy(
                    out=pair_planes[:, :, shift : shift + 2, 1, :].bitcast(I32),
                    in_=w_planes[:, :, first : first + 2 * QUARTER].rearrange("p g (s c) -> p g s c", s=2).bitcast(I32),
                )

        def interleave(b):
            grouped = stage.tile([P, G, T, PACK], BF16, align_bytes=64)
            if b == 0:
                for g, copy in ((0, nc.vector.tensor_copy), (1, nc.scalar.copy)):
                    copy(out=grouped[:, g], in_=raw[:, b, g].rearrange("p j t -> p t j"))
            else:
                nc.scalar.copy(
                    out=grouped[:].rearrange("p g (c i) j -> p g c j i", i=4),
                    in_=raw[:, b].rearrange("p g j (c i) -> p g c j i", i=4),
                )
            return grouped

        def shift_in_h(grouped, copy):
            flat = grouped[:].rearrange("p g t j -> p (g t j)").bitcast(F32)
            shifted = stage.tile([P, 2, G, T * PACK], BF16, align_bytes=64)
            h_minus, h_plus = words_of(shifted)
            copy(out=h_minus[:, TOKEN_WORDS:WORDS], in_=flat[:, 0 : WORDS - TOKEN_WORDS])
            copy(out=h_plus[:, 0 : WORDS - TOKEN_WORDS], in_=flat[:, TOKEN_WORDS:WORDS])
            return shifted

        def words_of(shifted):
            return [shifted[:, i].rearrange("p g k -> p (g k)").bitcast(F32) for i in range(2)]

        def set_edges(grouped, shifted, copy):
            flat = grouped[:].rearrange("p g t j -> p (g t j)").bitcast(F32)
            for moved, h in zip(words_of(shifted), (0, H - 1)):
                edge_of = lambda words: words.rearrange("p (r k) -> p r k", k=TOKEN_WORDS * H)[:, :, TOKEN_WORDS * h : TOKEN_WORDS * (h + 1)]
                copy(out=edge_of(moved), in_=edge_of(flat))

        def quantise_same(b, grouped):
            for g in range(G):
                nc.vector.quantize_mx(
                    out=x_words(SAME, b, g).bitcast(FP8X4),
                    scales=x_scales(SAME, b, g),
                    in_=grouped[:, g].rearrange("p t j -> p (t j)"),
                )

        def quantise_shifted(b, shifted):
            nc.vector.quantize_mx(
                out=h_words[:, b].rearrange("p v g t -> p (v g t)").bitcast(FP8X4),
                scales=h_planes[:, b].rearrange("p v g t -> p (v g t)"),
                in_=shifted[:].rearrange("p v g k -> p (v g k)"),
            )

        def move_rows(batches):
            def as_rows(tile, rows):
                return tile[:, batches].rearrange("p b g k -> p (b g k)").bitcast(I32).rearrange("p (r w k) -> p r w k", r=G * len(range(B)[batches]), w=rows)

            rows = as_rows(row_words, W + 2)
            nc.vector.tensor_copy(out=rows[:, :, 0 : W + 2 : W + 1, :], in_=rows[:, :, 1 : W + 1 : W - 1, :])
            same = as_rows(same_planes, W)
            both = as_rows(w_shift_planes, 2 * W)
            nc.vector.tensor_copy(out=both[:, :, 1:W, :], in_=same[:, :, 0 : W - 1, :])
            nc.vector.tensor_copy(out=both[:, :, W : 2 * W - 1, :], in_=same[:, :, 1:W, :])
            nc.vector.tensor_copy(out=both[:, :, 0 : 2 * W : 2 * W - 1, :], in_=same[:, :, 0 : W : W - 1, :])

        def product(b, version, words, planes):
            acc = banks.tile([P, BANK], F32, name="acc")
            for g in range(G):
                nc.tensor.matmul_mx(
                    out=acc[:],
                    lhsT=x_words(version, b, g).bitcast(FP8X4),
                    lhsT_scale=x_scales(version, b, g),
                    rhs=words[g].bitcast(FP4X4),
                    rhs_scale=planes[g],
                    start=(g == 0),
                    stop=(g == G - 1),
                )
            return acc

        def store_quarters(b, y12, first, last):
            rows = slice(b * T, (b + 1) * T)
            for out, branch, quarter in ((out_0, 0, first), (out_1, 4, x2_quarter(first))):
                n = last - first
                nc.sync.dma_start(
                    out=out.rearrange("b w h c -> (b w h) c")[rows, quarter * QUARTER : (quarter + n) * QUARTER],
                    in_=y12[:, branch + quarter : branch + quarter + n, :].rearrange("p q c -> p (q c)"),
                )

        def project_batch(b):
            rows = slice(b * T, (b + 1) * T)
            y3 = results.tile([P, C], F32)
            for c0 in range(0, C, BANK):
                acc = product(
                    b,
                    SAME,
                    [x3_words[:, g, 2 * c0 : 2 * (c0 + BANK)] for g in range(G)],
                    [w_planes[:, g, 2 * C + c0 : 2 * C + c0 + BANK] for g in range(G)],
                )
                nc.vector.tensor_tensor(
                    out=y3[:, c0 : c0 + BANK],
                    in0=acc[:],
                    in1=bias_rows[:, (2 * C + c0) // QUARTER : (2 * C + c0 + BANK) // QUARTER, :].rearrange("p q c -> p (q c)"),
                    op=ADD,
                )
            nc.sync.dma_start(out=out_2.rearrange("b w h c -> (b w h) c")[rows, :], in_=y3[:])

            y12 = results.tile([P, 8, QUARTER], F32)
            z = sums.tile([P, C], F32)
            for shift in SHIFTS:
                acc = product(
                    b,
                    shift,
                    [pair_words[:, g, shift].rearrange("p n k -> p (n k)") for g in range(G)],
                    [pair_planes[:, g, shift].rearrange("p n c -> p (n c)") for g in range(G)],
                )
                second = 4 + x2_quarter(shift)
                both = slice(shift, second + 1, second - shift)
                nc.vector.tensor_tensor(
                    out=y12[:, both, :],
                    in0=acc[:].rearrange("p (n c) -> p n c", n=2),
                    in1=bias_rows[:, both, :],
                    op=ADD,
                )
                if b == B - 1:
                    quarter = slice(shift * QUARTER, (shift + 1) * QUARTER)
                    engine = nc.gpsimd if shift < 2 else nc.vector
                    engine.tensor_tensor(out=z[:, quarter], in0=y3[:, quarter], in1=y12[:, shift, :], op=ADD)
                    if shift >= 1:
                        first = 0 if shift == 1 else shift
                        store_quarters(b, y12, first, shift + 1)
                if shift == QUANTISE_AFTER and b + AHEAD < B:
                    pair = slice(1, 2) if b == 0 else slice(b + 1, b + 3) if b % 2 else None
                    if pair:
                        for k in range(B)[pair]:
                            quantise_same(k, grouped[k])
                    quantise_shifted(b + AHEAD, shifted[b + AHEAD])
                    if pair:
                        move_rows(pair)
                    later = b + AHEAD + 1
                    if later < B:
                        shifted[later] = shift_in_h(grouped[later], nc.scalar.copy)
                        if later + 1 < B:
                            grouped[later + 1] = interleave(later + 1)
                        set_edges(grouped[later], shifted[later], nc.scalar.copy)
            y1 = y12[:, 0:4, :].rearrange("p q c -> p (q c)")
            y2 = y12[:, 4:8, :].rearrange("p q c -> p (q c)")
            if b < B - 1:
                nc.sync.dma_start(out=out_0.rearrange("b w h c -> (b w h) c")[rows, :], in_=y1)
                nc.sync.dma_start(out=out_1.rearrange("b w h c -> (b w h) c")[rows, :], in_=y2)
                nc.gpsimd.tensor_tensor(out=z[:], in0=y3[:], in1=y1, op=ADD)
            return y2, z[:]

        def sum_by_scalar(b, i, turned):
            nc.scalar.activation(
                out=unread[:, i, 0 : turned.shape[1]],
                in_=turned,
                func=COPY,
                accum_out=a_by_channel[:, b * BLOCKS + i : b * BLOCKS + i + 1],
            )

        def sum_tokens(b, parts):
            turned = [turns.tile([P, 2, 2, P], F32, name="turned") for quarter in range(4)]
            for n in range(2):
                for i in range(BLOCKS):
                    nc.tensor.transpose(turned[i // 2][:, i % 2, n, :], parts[n][:, i * P : (i + 1) * P], identity[:])
            for i in range(BLOCKS):
                sum_by_scalar(b, i, turned[i // 2][:, i % 2].rearrange("p n t -> p (n t)"))

        def turn_and_add(out, parts, i):
            for n in range(2):
                nc.tensor.matmul(
                    out=out,
                    lhsT=parts[n][:, i * P : (i + 1) * P],
                    rhs=identity[:],
                    is_transpose=True,
                    start=(n == 0),
                    stop=(n == 1),
                )

        def sum_tokens_at_end(b, parts):
            if b < B - 1:
                turned = [turns.tile([P, 4, P], F32, name="turned") for half in range(2)]
                for i in range(BLOCKS):
                    turn_and_add(turned[i // 4][:, i % 4, :], parts, i)
                for i in range(BLOCKS):
                    sum_by_scalar(b, i, turned[i // 4][:, i % 4, :])
                return
            turned = [banks.tile([P, 2, P], F32, name="acc") for quarter in range(4)]
            for quarter in QUARTER_ORDER:
                for i in range(2):
                    turn_and_add(turned[quarter][:, i, :], parts, 2 * quarter + i)
            for quarter in QUARTER_ORDER:
                if quarter == QUARTER_ORDER[-1]:
                    first = b * BLOCKS + 2 * quarter
                    nc.vector.tensor_reduce(
                        out=a_by_channel[:, first : first + 2], in_=turned[quarter][:], op=ADD, axis=mybir.AxisListType.X
                    )
                    continue
                for i in range(2):
                    sum_by_scalar(b, 2 * quarter + i, turned[quarter][:, i, :])

        ctx.enter_context(tc.manual_schedule())
        grouped, shifted = {}, {}
        keep_tensor_busy()
        spread = {branch: spread_bias(branch) for branch in (2, 0, 1)}
        grouped[0] = interleave(0)
        quantise_same(0, grouped[0])
        shifted[0] = shift_in_h(grouped[0], nc.vector.tensor_copy)
        move_rows(slice(0, 1))
        set_edges(grouped[0], shifted[0], nc.vector.tensor_copy)
        keep_bias(2, spread[2], nc.scalar.copy)
        quantise_shifted(0, shifted[0])
        pair_scale_bytes()
        keep_bias(0, spread[0], nc.scalar.copy)
        keep_bias(1, spread[1], nc.scalar.copy)
        grouped[1] = interleave(1)
        shifted[1] = shift_in_h(grouped[1], nc.scalar.copy)
        set_edges(grouped[1], shifted[1], nc.scalar.copy)
        grouped[2] = interleave(2)
        parts_of_batch = []
        for b in range(B):
            parts_of_batch.append(project_batch(b))
            if b >= LATE:
                (sum_tokens if b < B - 1 else sum_tokens_at_end)(b - LATE, parts_of_batch[b - LATE])
        for b in range(B - LATE, B):
            sum_tokens_at_end(b, parts_of_batch[b])

        a_turned = turns.tile([P, P], F32, tag="turned")
        nc.tensor.transpose(a_turned[:], a_by_channel[:], identity[:])
        nc.scalar.copy(out=a_rows[:], in_=a_turned[:])
        nc.sync.dma_start(
            out=out_3.rearrange("b (i c) -> (b i) c", c=P),
            in_=a_rows[0 : B * BLOCKS, :],
        )
